import numpy as np
import ml_dtypes


def mxq(x, axis, fmt="e4m3"):
    dtype, down = {"e4m3": (ml_dtypes.float8_e4m3fn, 7), "e5m2": (ml_dtypes.float8_e5m2, 14)}[fmt]
    v = np.moveaxis(np.asarray(x, np.float32).astype(ml_dtypes.bfloat16).astype(np.float64), axis, -1)
    blocks = v.reshape(v.shape[:-1] + (-1, 32))
    amax = np.abs(blocks).max(-1, keepdims=True)
    byte = np.maximum(np.where(amax > 0, np.frexp(amax)[1] - 1 + 127, 0) - down, 1)
    scale = np.exp2(byte - 127.0)
    codes = (blocks / scale).astype(np.float32).astype(dtype).astype(np.float64)
    return np.moveaxis((codes * scale).reshape(v.shape), -1, axis)


WIDE = False


def mx_kscale(k):
    if not WIDE:
        return np.ones(k)
    levels = np.array([18, -18])
    if k % 512:
        return np.exp2(np.random.permutation(np.resize(levels, k // 32))).repeat(32)
    a = np.empty((k // 512, 16))
    for p in range(k // 512):
        a[p, :8] = np.random.permutation(np.resize(levels, 8))
        for g in range(8):
            far = levels[np.abs(levels - a[p, g]) >= 10]
            a[p, g + 8] = far[np.random.randint(len(far))]
    return np.exp2(a.ravel()).repeat(32)


BF16 = ml_dtypes.bfloat16


def bf(x):
    return np.asarray(x, np.float32).astype(BF16)


def f64(x):
    return np.asarray(x).astype(np.float64)


B, U = 1024, 1024
MASK_DENSITY = 1.0 / 16.0
W_STD = 1.0 / np.sqrt(U * MASK_DENSITY)


def setup_inputs():
    s = mx_kscale(B)[:, None]
    u = mx_kscale(U)
    v = mx_kscale(U)
    h0_0 = bf(np.random.standard_normal((B, U)))
    k1_0 = bf(np.random.standard_normal((U, U)) * W_STD)
    k2_0 = bf(np.random.standard_normal((U, U)) * W_STD)
    m1 = bf(np.random.random((U, U)) < MASK_DENSITY)
    m2 = bf(np.random.random((U, U)) < MASK_DENSITY)
    scaling = bf(np.random.uniform(1.25, 1.75, 1))
    bias = bf(np.random.standard_normal(U) * 0.5)
    g = bf(np.random.standard_normal((B, U)) * np.exp2(np.random.randint(-6, 1, (B, 1))) / s * u)
    h1 = f64(h0_0) @ (f64(k1_0) * f64(m1))
    z = f64(scaling) * (h1 @ (f64(k2_0) * f64(m2))) + f64(bias)
    return {"h0": bf(f64(h0_0) * s),
            "k1": bf(f64(k1_0) / v),
            "k2": bf(f64(k2_0) * v[:, None] / u),
            "m1": m1,
            "m2": m2,
            "scaling": scaling,
            "bias": bias,
            "z": np.asarray(z, np.float32),
            "grad_out": g}


def reference(h0, k1, k2, m1, m2, scaling, bias, z, grad_out):
    m1f = f64(m1)
    w1 = f64(k1) * m1f
    w2 = f64(k2) * f64(m2)
    dz2 = f64(grad_out) * (f64(z) > 0.0) * f64(scaling)
    dz1 = mxq(dz2, 1, "e5m2") @ mxq(w2, 1, "e4m3").T
    dh0 = mxq(dz1, 1, "e5m2") @ mxq(w1, 1, "e4m3").T
    dw1 = mxq(f64(h0), 0, "e4m3").T @ mxq(dz1, 0, "e5m2")
    return dh0, dw1 * m1f

@@ -1,0 +1,426 @@
+from contextlib import ExitStack
+
+import concourse.mybir as mybir
+from concourse.masks import make_identity
+
+FLOPS = 3 * 2 * 1024 * 1024 * 1024
+
+F32 = mybir.dt.float32
+BF16 = mybir.dt.bfloat16
+U32 = mybir.dt.uint32
+U8 = mybir.dt.uint8
+E4 = mybir.dt.float8_e4m3fn_x4
+E5 = mybir.dt.float8_e5m2_x4
+ALU = mybir.AluOpType
+
+P = 128
+U = 1024
+HALF = 512
+
+
+def tile_sparsefactorisationdense_pa_v_kernel(
+    tc, h0, k1, k2, m1, m2, scaling, bias, z, grad_out, out_0, out_1
+):
+    nc = tc.nc
+    k1_v = k1.rearrange("(c p a) w -> c p a w", a=4, p=P)
+    k2_v = k2.rearrange("(c p a) w -> c p a w", a=2, p=P)
+    m1_v = m1.rearrange("(c p a) w -> c p a w", a=4, p=P)
+    m2_v = m2.rearrange("(c p a) w -> c p a w", a=2, p=P)
+    z_v = z.rearrange("(b p s) w -> b p s w", p=P, s=4)
+    g_v = grad_out.rearrange("(b p s) w -> b p s w", p=P, s=4)
+    h_v = h0.rearrange("(b p s) w -> b p s w", p=P, s=4)
+    out_0_v = out_0.rearrange("(b p s) w -> b p s w", p=P, s=4)
+    out_1_v = out_1.rearrange("(c p a) w -> c p a w", a=4, p=P)
+
+    with ExitStack() as ctx:
+        const = ctx.enter_context(tc.tile_pool(name="const", bufs=1))
+        raw8 = ctx.enter_context(tc.tile_pool(name="raw8", bufs=3))
+        plains = ctx.enter_context(tc.tile_pool(name="plains", bufs=2))
+        raw_h = ctx.enter_context(tc.tile_pool(name="raw_h", bufs=3))
+        raw4 = ctx.enter_context(tc.tile_pool(name="raw4", bufs=14))
+        mask_pool = ctx.enter_context(tc.tile_pool(name="masks", bufs=1))
+        mid = ctx.enter_context(tc.tile_pool(name="mid", bufs=2))
+        grps = ctx.enter_context(tc.tile_pool(name="grps", bufs=3))
+        keep = ctx.enter_context(tc.tile_pool(name="keep", bufs=1))
+        ps_t = ctx.enter_context(tc.psum_pool(name="ps_t", bufs=3))
+        ps_m = ctx.enter_context(tc.psum_pool(name="ps_m", bufs=5))
+
+        ident = const.tile([P, P], F32, name="ident")
+        make_identity(nc, ident[:])
+        ones = const.tile([P, P], BF16, name="ones")
+        nc.gpsimd.memset(ones[:], 1.0)
+        gain_in = const.tile([P, 1], BF16, name="gain_in")
+        nc.scalar.dma_start(out=gain_in[0:1, :], in_=scaling.rearrange("(p w) -> p w", p=1))
+        gain_row = const.tile([P, 64], BF16, name="gain_row")
+        nc.gpsimd.memset(gain_row[:], 0.0)
+        gain = const.tile([P, 1], F32, name="gain")
+
+        def codes(name, dims):
+            return (
+                keep.tile([P] + dims, U32, align_bytes=64, name=name + "_q"),
+                keep.tile([P] + dims, U8, align_bytes=64, name=name + "_s"),
+            )
+
+        w2_q, w2_s = codes("w2", [2, 2, HALF])
+        w1_q, w1_s = codes("w1", [2, 2, HALF])
+        z2_q, z2_s = codes("z2", [4, 2, 2, P])
+        db_q, db_s = codes("db", [2, 2, HALF])
+        h_q, h_s = codes("h", [2, 2, HALF])
+        dz1 = [keep.tile([P, 4, U], BF16, align_bytes=64, name="dz1_%d" % b) for b in range(2)]
+
+        def new_grp(width):
+            return grps.tile([P, width], BF16, align_bytes=64, name="grp")
+
+        def load(pool, name, shape, dtype, src):
+            t = pool.tile([P] + shape, dtype, name=name)
+            nc.sync.dma_start(out=t[:], in_=src)
+            return t
+
+        def sort_mult(dst, a, b):
+            nc.vector.tensor_tensor(
+                out=dst.rearrange("p u a (q r) -> p u (a q) r", r=16),
+                in0=a.rearrange("p a (q u r) -> p u (a q) r", u=2, r=16),
+                in1=b.rearrange("p a (q u r) -> p u (a q) r", u=2, r=16),
+                op=ALU.mult,
+            )
+
+        def leave(out, in_, on):
+            if on == "DVE":
+                nc.vector.tensor_copy(out=out, in_=in_)
+            else:
+                nc.scalar.copy(out=out, in_=in_)
+
+        def turn2(tr, k, half):
+            for u in range(2):
+                nc.tensor.transpose(tr[:, k + u, :], half(u).bitcast(F32), ident[:])
+
+        def mx(acc, lq, ls, rq, rs, ldt, rdt):
+            for g in range(2):
+                nc.tensor.matmul_mx(
+                    out=acc[:],
+                    lhsT=lq[g].bitcast(ldt),
+                    lhsT_scale=ls[g],
+                    rhs=rq[g].bitcast(rdt),
+                    rhs_scale=rs[g],
+                    start=(g == 0),
+                    stop=(g == 1),
+                )
+
+        prod, grp = {}, {}
+        k_sb, m_sb, z_sb, g_sb, h_sb = {}, {}, {}, {}, {}
+        codes_of = {1: (w1_q, w1_s), 2: (w2_q, w2_s)}
+
+        def wm(f, c):
+            rows = 2 if f == 2 else 4
+            w_sb = mid.tile([P, 2, rows, HALF], BF16, name="w_sb")
+            if f == 2 and c == 0:
+                for a in range(2):
+                    sort_mult(w_sb[:, :, a : a + 1, :], k_sb[f, c, a][:], m_sb[f, c, a][:])
+            else:
+                sort_mult(w_sb[:], k_sb[f, c][:], m_sb[f, c][:])
+            prod["w", f, c] = w_sb
+
+        def wt(f, c, on=("ACT", "ACT")):
+            half = c // 2
+            w_sb, a0 = (prod["w", 2, c], 0) if f == 2 else (prod["w", 1, half], 2 * (c % 2))
+            if (f, half) not in grp:
+                grp[f, half] = new_grp(4096)
+            for g in range(2):
+                tr = ps_t.tile([P, 4, P], F32, name="tr")
+                for a in range(2):
+                    turn2(tr, 2 * a, lambda u: w_sb[:, u, a0 + a, 256 * g : 256 * g + 256])
+                words = grp[f, half][:].bitcast(F32)[:, 1024 * g : 1024 * g + 1024]
+                if f == 2:
+                    lo = 512 * (c % 2)
+                    dst = words[:, lo : lo + 512].rearrange("p (r a u) -> p r a u", a=2, u=2)
+                else:
+                    dst = words.rearrange("p (r a u) -> p r a u", a=4, u=2)[:, :, a0 : a0 + 2, :]
+                leave(dst, tr[:].rearrange("p (a u) r -> p r a u", u=2), on[g])
+
+        def wq(f, half):
+            q, s = codes_of[f]
+            nc.vector.quantize_mx(
+                out=q[:, half].rearrange("p g c -> p (g c)").bitcast(E4),
+                scales=s[:, half].rearrange("p g c -> p (g c)"),
+                in_=grp[f, half][:],
+            )
+
+        def s_turn(dst, src, on):
+            for i in range(2):
+                tr = ps_t.tile([P, 4, P], F32, name="tr")
+                for g in range(2):
+                    turn2(tr, 2 * g, lambda u: src(i, g, u))
+                leave(
+                    dst.bitcast(F32)[:, 512 * i : 512 * i + 512].rearrange("p (g r u) -> p g r u", g=2, u=2),
+                    tr[:].rearrange("p (g u) r -> p g r u", u=2),
+                    on[i],
+                )
+
+        def s_quant(src, n0, n1):
+            nc.vector.quantize_mx(
+                out=z2_q[:, n0:n1].rearrange("p n s g c -> p (n s g c)").bitcast(E5),
+                scales=z2_s[:, n0:n1].rearrange("p n s g c -> p (n s g c)"),
+                in_=src,
+            )
+
+        def zs(n):
+            mask = mask_pool.tile([P, 2, U], BF16, name="mask")
+            nc.vector.tensor_scalar(out=mask[:], in0=z_sb[n][:], scalar1=0.0, scalar2=gain[:], op0=ALU.is_gt, op1=ALU.mult)
+            prod["mask", n] = mask
+
+        def zm(n):
+            w_sb = mid.tile([P, 2, 2, HALF], BF16, name="w_sb")
+            sort_mult(w_sb[:], g_sb[n][:], prod["mask", n][:])
+            prod["z", n] = w_sb
+
+        def zt(n, on=("ACT", "ACT")):
+            grp["z", n] = mid.tile([P, 2048], BF16, align_bytes=64, name="gz")
+            s_turn(grp["z", n][:], lambda i, g, u: prod["z", n][:, u, i, 256 * g : 256 * g + 256], on)
+
+        def zq(n):
+            s_quant(grp["z", n][:], n, n + 1)
+
+        def p1(n, i, jh, on="ACT"):
+            acc = ps_m.tile([P, HALF], F32, name="acc")
+            mx(acc, [z2_q[:, n, i, g, :] for g in range(2)], [z2_s[:, n, i, g, :] for g in range(2)],
+               [w2_q[:, jh, g, :] for g in range(2)], [w2_s[:, jh, g, :] for g in range(2)], E5, E4)
+            leave(
+                dz1[n // 2][:, 2 * (n % 2) + i, HALF * jh : HALF * jh + HALF].rearrange("p (u q r) -> p u q r", u=2, q=16),
+                acc[:].rearrange("p (q u r) -> p u q r", u=2, q=16),
+                on,
+            )
+
+        def tt(n, on=("ACT", "ACT")):
+            def part(i, g, u):
+                lo = HALF * g + 256 * u
+                return dz1[n // 2][:, 2 * (n % 2) + i, lo : lo + 256]
+
+            if ("t", n // 2) not in grp:
+                grp["t", n // 2] = new_grp(4096)
+            lo = 2048 * (n % 2)
+            s_turn(grp["t", n // 2][:, lo : lo + 2048], part, on)
+
+        def tq(b):
+            s_quant(grp["t", b][:], 2 * b, 2 * b + 2)
+
+        def bl(b, jh, on="DVE"):
+            grp["b", b, jh] = mid.tile([P, 2048], BF16, align_bytes=64, name="grb")
+            src = dz1[b][:, :, HALF * jh : HALF * jh + HALF]
+            leave(
+                grp["b", b, jh][:].rearrange("p (c i s) -> p c s i", s=4, i=4),
+                src.rearrange("p s (c i) -> p c s i", i=4),
+                on,
+            )
+
+        def bq(b, jh):
+            nc.vector.quantize_mx(out=db_q[:, b, jh, :].bitcast(E5), scales=db_s[:, b, jh, :], in_=grp["b", b, jh][:])
+
+        def hl(b, ih, on="DVE"):
+            if ("h", b) not in grp:
+                grp["h", b] = new_grp(4096)
+            dst = grp["h", b][:, 2048 * ih : 2048 * ih + 2048]
+            src = h_sb[b][:, :, HALF * ih : HALF * ih + HALF].rearrange("p s (c a) -> p a c s", a=4)
+            leave(dst.rearrange("p (a c s) -> p a c s", a=4, s=4), src, on)
+
+        def hq(b):
+            nc.vector.quantize_mx(
+                out=h_q[:, b].rearrange("p h c -> p (h c)").bitcast(E4),
+                scales=h_s[:, b].rearrange("p h c -> p (h c)"),
+                in_=grp["h", b][:],
+            )
+
+        def p3(it, jh, on="DVE"):
+            half, a = it // 4, it % 4
+            if ("res3", it) not in prod:
+                prod["res3", it] = raw4.tile([P, U], F32, name="r4")
+            res = prod["res3", it]
+            lo = P * a
+            acc = ps_m.tile([P, HALF], F32, name="acc")
+            mx(acc, [h_q[:, b, half, lo : lo + P] for b in range(2)], [h_s[:, b, half, lo : lo + P] for b in range(2)],
+               [db_q[:, b, jh, :] for b in range(2)], [db_s[:, b, jh, :] for b in range(2)], E4, E5)
+            cols = slice(HALF * jh, HALF * jh + HALF)
+            unsorted = acc[:].rearrange("p (u q r) -> p q u r", u=2, q=16)
+            if on == "DVE":
+                nc.vector.tensor_tensor(
+                    out=res[:, cols].rearrange("p (q u r) -> p q u r", u=2, q=16),
+                    in0=unsorted,
+                    in1=m_sb[1, half][:, a, cols].rearrange("p (q u r) -> p q u r", u=2, q=16),
+                    op=ALU.mult,
+                )
+            else:
+                plain = plains.tile([P, HALF], F32, name="plain")
+                nc.scalar.copy(out=plain[:].rearrange("p (q u r) -> p q u r", u=2, q=16), in_=unsorted)
+                nc.gpsimd.tensor_tensor(out=res[:, cols], in0=plain[:], in1=m_sb[1, half][:, a, cols], op=ALU.mult)
+
+        def s3(it):
+            nc.sync.dma_start(out=out_1_v[it // 4][:, it % 4, :], in_=prod["res3", it][:])
+
+        def p2(half, n, i, on="ACT"):
+            if ("res2", half, n) not in prod:
+                prod["res2", half, n] = raw4.tile([P, 2, HALF], F32, name="r4")
+            acc = ps_m.tile([P, HALF], F32, name="acc")
+            mx(acc, [z2_q[:, n, i, g, :] for g in range(2)], [z2_s[:, n, i, g, :] for g in range(2)],
+               [w1_q[:, half, g, :] for g in range(2)], [w1_s[:, half, g, :] for g in range(2)], E5, E4)
+            leave(prod["res2", half, n][:, i, :], acc[:], on)
+
+        def s2(half, n):
+            b, s0 = n // 2, 2 * (n % 2)
+            nc.sync.dma_start(out=out_0_v[b][:, s0 : s0 + 2, HALF * half : HALF * half + HALF], in_=prod["res2", half, n][:])
+
+        def ld(kind, i):
+            if kind == "w":
+                if i == 0:
+                    for a in range(2):
+                        k_sb[2, 0, a] = load(raw4, "r4", [1, U], BF16, k2_v[0][:, a : a + 1, :])
+                        m_sb[2, 0, a] = load(raw4, "r4", [1, U], BF16, m2_v[0][:, a : a + 1, :])
+                else:
+                    k_sb[2, i] = load(raw4, "r4", [2, U], BF16, k2_v[i])
+                    m_sb[2, i] = load(raw4, "r4", [2, U], BF16, m2_v[i])
+            elif kind == "z":
+                b, s0 = i // 2, 2 * (i % 2)
+                z_sb[i] = load(raw8, "r8", [2, U], F32, z_v[b][:, s0 : s0 + 2, :])
+                g_sb[i] = load(raw4, "r4", [2, U], BF16, g_v[b][:, s0 : s0 + 2, :])
+            elif kind == "h":
+                h_sb[i] = load(raw_h, "hm", [4, U], BF16, h_v[i])
+            elif kind == "m":
+                m_sb[1, i] = load(raw_h, "hm", [4, U], BF16, m1_v[i])
+            else:
+                k_sb[1, i] = load(raw8, "r8", [4, U], BF16, k1_v[i])
+
+        ld("w", 2)
+        ld("z", 0)
+        ld("w", 0)
+        ld("w", 3)
+        ld("w", 1)
+        ld("z", 1)
+        ld("z", 3)
+        ld("z", 2)
+        ld("h", 0)
+        ld("m", 1)
+        ld("k", 1)
+        ld("k", 0)
+        ld("m", 0)
+        ld("h", 1)
+        with tc.manual_schedule():
+            nc.scalar.copy(out=gain_row[0:1, 0:1], in_=gain_in[0:1, :])
+            spread = ps_m.tile([P, HALF], F32, name="acc")
+            nc.tensor.matmul(spread[:, 0:64], lhsT=ones[:], rhs=gain_row[:], start=True, stop=True)
+            nc.scalar.copy(out=gain[:], in_=spread[:, 0:1])
+            wm(2, 2)
+            zs(0)
+            wt(2, 2, ("ACT", "ACT"))
+            zm(0)
+            zt(0)
+            wm(2, 0)
+            zq(0)
+            wm(2, 3)
+            wt(2, 0, ("DVE", "ACT"))
+            wt(2, 3)
+            wm(2, 1)
+            wt(2, 1)
+            wq(2, 1)
+            zs(1)
+            p1(0, 1, 1)
+            zm(1)
+            p1(0, 0, 1)
+            wq(2, 0)
+            zt(1)
+            p1(0, 0, 0)
+            zs(3)
+            zq(1)
+            p1(0, 1, 0)
+            tt(0)
+            zm(3)
+            p1(1, 1, 1)
+            zs(2)
+            zm(2)
+            zt(3)
+            p1(1, 1, 0, "DVE")
+            p1(1, 0, 1)
+            p1(1, 0, 0)
+            zq(3)
+            zt(2)
+            hl(0, 1)
+            bl(0, 0, "ACT")
+            hl(0, 0)
+            p1(3, 0, 0)
+            p1(3, 1, 1)
+            zq(2)
+            hq(0)
+            p1(3, 1, 0)
+            wm(1, 1)
+            tt(1)
+            p1(2, 1, 1, "DVE")
+            p1(2, 0, 1, "DVE")
+            p1(3, 0, 1)
+            p1(2, 1, 0, "DVE")
+            tq(0)
+            p1(2, 0, 0)
+            wm(1, 0)
+            wt(1, 2)
+            wt(1, 3)
+            tt(2)
+            wq(1, 1)
+            tt(3, ("ACT", "DVE"))
+            hl(1, 0, "ACT")
+            wt(1, 1)
+            p2(1, 0, 0)
+            hl(1, 1)
+            p2(1, 0, 1)
+            tq(1)
+            bl(1, 0)
+            wt(1, 0)
+            bq(0, 0)
+            p2(1, 1, 0, "DVE")
+            wq(1, 0)
+            bq(1, 0)
+            s2(1, 0)
+            p2(1, 1, 1)
+            p2(1, 3, 0)
+            p2(1, 3, 1)
+            hq(1)
+            bl(0, 1)
+            bl(1, 1)
+            p2(1, 2, 1)
+            s2(1, 1)
+            p2(1, 2, 0)
+            bq(0, 1)
+            p2(0, 3, 0)
+            p2(0, 3, 1)
+            s2(1, 3)
+            p2(0, 0, 0)
+            p2(0, 0, 1)
+            s2(1, 2)
+            p2(0, 1, 0)
+            p2(0, 1, 1)
+            bq(1, 1)
+            s2(0, 3)
+            s2(0, 0)
+            p2(0, 2, 1)
+            p2(0, 2, 0)
+            p3(4, 0)
+            p3(6, 0, "ACT")
+            p3(4, 1)
+            p3(6, 1)
+            s2(0, 1)
+            s2(0, 2)
+            p3(3, 1)
+            p3(2, 1, "ACT")
+            p3(3, 0)
+            p3(2, 0)
+            p3(7, 0)
+            p3(0, 1, "ACT")
+            s3(4)
+            s3(6)
+            p3(7, 1)
+            p3(0, 0)
+            p3(1, 1)
+            p3(1, 0)
+            s3(3)
+            p3(5, 0)
+            p3(5, 1)
+            s3(2)
+            s3(7)
+            s3(0)
+            s3(1)
+            s3(5)

@@ -16,34 +16,31 @@ ALU = mybir.AluOpType
 P = 128
 U = 1024
 HALF = 512
+GROUP = 2048
 
 
 def tile_sparsefactorisationdense_pa_v_kernel(
     tc, h0, k1, k2, m1, m2, scaling, bias, z, grad_out, out_0, out_1
 ):
     nc = tc.nc
-    k1_v = k1.rearrange("(c p a) w -> c p a w", a=4, p=P)
-    k2_v = k2.rearrange("(c p a) w -> c p a w", a=2, p=P)
-    m1_v = m1.rearrange("(c p a) w -> c p a w", a=4, p=P)
-    m2_v = m2.rearrange("(c p a) w -> c p a w", a=2, p=P)
-    z_v = z.rearrange("(b p s) w -> b p s w", p=P, s=4)
-    g_v = grad_out.rearrange("(b p s) w -> b p s w", p=P, s=4)
-    h_v = h0.rearrange("(b p s) w -> b p s w", p=P, s=4)
-    out_0_v = out_0.rearrange("(b p s) w -> b p s w", p=P, s=4)
-    out_1_v = out_1.rearrange("(c p a) w -> c p a w", a=4, p=P)
+
+    def by_slots(x):
+        return x.rearrange("(c p s) w -> c p s w", p=P, s=4)
+
+    k_v = {1: by_slots(k1), 2: by_slots(k2)}
+    m_v = {1: by_slots(m1), 2: by_slots(m2)}
+    z_v, g_v, h_v = by_slots(z), by_slots(grad_out), by_slots(h0)
+    out_0_v, out_1_v = by_slots(out_0), by_slots(out_1)
 
     with ExitStack() as ctx:
         const = ctx.enter_context(tc.tile_pool(name="const", bufs=1))
-        raw8 = ctx.enter_context(tc.tile_pool(name="raw8", bufs=3))
-        plains = ctx.enter_context(tc.tile_pool(name="plains", bufs=2))
-        raw_h = ctx.enter_context(tc.tile_pool(name="raw_h", bufs=3))
-        raw4 = ctx.enter_context(tc.tile_pool(name="raw4", bufs=14))
-        mask_pool = ctx.enter_context(tc.tile_pool(name="masks", bufs=1))
-        mid = ctx.enter_context(tc.tile_pool(name="mid", bufs=2))
-        grps = ctx.enter_context(tc.tile_pool(name="grps", bufs=3))
+        big = ctx.enter_context(tc.tile_pool(name="big", bufs=10))
+        small = ctx.enter_context(tc.tile_pool(name="small", bufs=10))
+        mask_pool = ctx.enter_context(tc.tile_pool(name="mask_pool", bufs=2))
+        prods = ctx.enter_context(tc.tile_pool(name="prods", bufs=3))
+        groups = ctx.enter_context(tc.tile_pool(name="groups", bufs=6))
         keep = ctx.enter_context(tc.tile_pool(name="keep", bufs=1))
-        ps_t = ctx.enter_context(tc.psum_pool(name="ps_t", bufs=3))
-        ps_m = ctx.enter_context(tc.psum_pool(name="ps_m", bufs=5))
+        psum = ctx.enter_context(tc.psum_pool(name="psum", bufs=8))
 
         ident = const.tile([P, P], F32, name="ident")
         make_identity(nc, ident[:])
@@ -55,372 +52,315 @@ def tile_sparsefactorisationdense_pa_v_kernel(
         nc.gpsimd.memset(gain_row[:], 0.0)
         gain = const.tile([P, 1], F32, name="gain")
 
-        def codes(name, dims):
+        def codes(name):
             return (
-                keep.tile([P] + dims, U32, align_bytes=64, name=name + "_q"),
-                keep.tile([P] + dims, U8, align_bytes=64, name=name + "_s"),
+                keep.tile([P, 4, HALF], U32, align_bytes=64, name=name + "_q"),
+                keep.tile([P, 4, HALF], U8, align_bytes=64, name=name + "_s"),
             )
 
-        w2_q, w2_s = codes("w2", [2, 2, HALF])
-        w1_q, w1_s = codes("w1", [2, 2, HALF])
-        z2_q, z2_s = codes("z2", [4, 2, 2, P])
-        db_q, db_s = codes("db", [2, 2, HALF])
-        h_q, h_s = codes("h", [2, 2, HALF])
-        dz1 = [keep.tile([P, 4, U], BF16, align_bytes=64, name="dz1_%d" % b) for b in range(2)]
+        w_codes = {1: codes("w1"), 2: codes("w2")}
+        row_codes, db_codes, h_codes = codes("rows"), codes("db"), codes("h")
+        dz1 = {(b, jh): keep.tile([P, 4, HALF], BF16, name="dz1_%d%d" % (b, jh)) for b in range(2) for jh in range(2)}
 
-        def new_grp(width):
-            return grps.tile([P, width], BF16, align_bytes=64, name="grp")
+        def bank():
+            return psum.tile([P, HALF], F32, name="bank")
 
-        def load(pool, name, shape, dtype, src):
-            t = pool.tile([P] + shape, dtype, name=name)
+        def new_group():
+            return groups.tile([P, GROUP], BF16, align_bytes=64, name="group")
+
+        def load(pool, slots, dtype, src):
+            t = pool.tile([P, slots, U], dtype, name="raw")
             nc.sync.dma_start(out=t[:], in_=src)
             return t
 
-        def sort_mult(dst, a, b):
+        def sort_mult(a, b):
+            dst = prods.tile([P, 2, 2, HALF], BF16, name="prod")
             nc.vector.tensor_tensor(
-                out=dst.rearrange("p u a (q r) -> p u (a q) r", r=16),
+                out=dst[:].rearrange("p u a (q r) -> p u (a q) r", r=16),
                 in0=a.rearrange("p a (q u r) -> p u (a q) r", u=2, r=16),
                 in1=b.rearrange("p a (q u r) -> p u (a q) r", u=2, r=16),
                 op=ALU.mult,
             )
+            return dst
 
-        def leave(out, in_, on):
-            if on == "DVE":
+        def move(out, in_, on):
+            if on == "V":
                 nc.vector.tensor_copy(out=out, in_=in_)
             else:
                 nc.scalar.copy(out=out, in_=in_)
 
-        def turn2(tr, k, half):
-            for u in range(2):
-                nc.tensor.transpose(tr[:, k + u, :], half(u).bitcast(F32), ident[:])
+        def turn(parts):
+            tr = bank()
+            for k, part in enumerate(parts):
+                nc.tensor.transpose(tr[:, P * k : P * k + P], part.bitcast(F32), ident[:])
+            return tr
 
-        def mx(acc, lq, ls, rq, rs, ldt, rdt):
+        def quantize(pair, k, src, fmt):
+            nc.vector.quantize_mx(out=pair[0][:, k, :].bitcast(fmt), scales=pair[1][:, k, :], in_=src[:])
+
+        def product(left, left_fmt, right, right_fmt):
+            acc = bank()
             for g in range(2):
                 nc.tensor.matmul_mx(
                     out=acc[:],
-                    lhsT=lq[g].bitcast(ldt),
-                    lhsT_scale=ls[g],
-                    rhs=rq[g].bitcast(rdt),
-                    rhs_scale=rs[g],
+                    lhsT=left(0, g).bitcast(left_fmt),
+                    lhsT_scale=left(1, g),
+                    rhs=right(0, g).bitcast(right_fmt),
+                    rhs_scale=right(1, g),
                     start=(g == 0),
                     stop=(g == 1),
                 )
+            return acc
 
-        prod, grp = {}, {}
-        k_sb, m_sb, z_sb, g_sb, h_sb = {}, {}, {}, {}, {}
-        codes_of = {1: (w1_q, w1_s), 2: (w2_q, w2_s)}
+        raw, prod, grp, res = {}, {}, {}, {}
 
-        def wm(f, c):
-            rows = 2 if f == 2 else 4
-            w_sb = mid.tile([P, 2, rows, HALF], BF16, name="w_sb")
-            if f == 2 and c == 0:
-                for a in range(2):
-                    sort_mult(w_sb[:, :, a : a + 1, :], k_sb[f, c, a][:], m_sb[f, c, a][:])
-            else:
-                sort_mult(w_sb[:], k_sb[f, c][:], m_sb[f, c][:])
-            prod["w", f, c] = w_sb
+        def ld_w(f, half):
+            raw_m = load(big, 4, BF16, m_v[f][half])
+            raw_k = load(big, 4, BF16, k_v[f][half])
+            for pair in range(2):
+                raw["m", f, half, pair] = raw_m[:, 2 * pair : 2 * pair + 2, :]
+                raw["k", f, half, pair] = raw_k[:, 2 * pair : 2 * pair + 2, :]
 
-        def wt(f, c, on=("ACT", "ACT")):
-            half = c // 2
-            w_sb, a0 = (prod["w", 2, c], 0) if f == 2 else (prod["w", 1, half], 2 * (c % 2))
-            if (f, half) not in grp:
-                grp[f, half] = new_grp(4096)
+        def ld_w_pair(f, half, pair):
+            raw["m", f, half, pair] = load(small, 2, BF16, m_v[f][half][:, 2 * pair : 2 * pair + 2, :])[:]
+            raw["k", f, half, pair] = load(small, 2, BF16, k_v[f][half][:, 2 * pair : 2 * pair + 2, :])[:]
+
+        def ld_z(n):
+            lo = 2 * (n % 2)
+            raw["z", n] = load(big, 2, F32, z_v[n // 2][:, lo : lo + 2, :])
+            raw["g", n] = load(small, 2, BF16, g_v[n // 2][:, lo : lo + 2, :])
+
+        def ld_h(b):
+            raw["h", b] = load(big, 4, BF16, h_v[b])
+
+        def wm(f, half, pair):
+            prod["w", f, half, pair] = sort_mult(raw["k", f, half, pair], raw["m", f, half, pair])
+
+        def wt(f, half, pair, on="SS"):
+            src = prod["w", f, half, pair]
             for g in range(2):
-                tr = ps_t.tile([P, 4, P], F32, name="tr")
-                for a in range(2):
-                    turn2(tr, 2 * a, lambda u: w_sb[:, u, a0 + a, 256 * g : 256 * g + 256])
-                words = grp[f, half][:].bitcast(F32)[:, 1024 * g : 1024 * g + 1024]
-                if f == 2:
-                    lo = 512 * (c % 2)
-                    dst = words[:, lo : lo + 512].rearrange("p (r a u) -> p r a u", a=2, u=2)
-                else:
-                    dst = words.rearrange("p (r a u) -> p r a u", a=4, u=2)[:, :, a0 : a0 + 2, :]
-                leave(dst, tr[:].rearrange("p (a u) r -> p r a u", u=2), on[g])
+                if pair == 0:
+                    grp["w", f, half, g] = new_group()
+                tr = turn([src[:, u, a, 256 * g : 256 * g + 256] for a in range(2) for u in range(2)])
+                words = grp["w", f, half, g][:].bitcast(F32).rearrange("p (r a u) -> p r a u", a=4, u=2)
+                move(words[:, :, 2 * pair : 2 * pair + 2, :], tr[:].rearrange("p (a u r) -> p r a u", a=2, u=2), on[g])
 
         def wq(f, half):
-            q, s = codes_of[f]
-            nc.vector.quantize_mx(
-                out=q[:, half].rearrange("p g c -> p (g c)").bitcast(E4),
-                scales=s[:, half].rearrange("p g c -> p (g c)"),
-                in_=grp[f, half][:],
-            )
+            for g in range(2):
+                quantize(w_codes[f], 2 * half + g, grp["w", f, half, g], E4)
 
-        def s_turn(dst, src, on):
+        def rows_turn(kind, n, part, on):
+            grp[kind, n] = new_group()
             for i in range(2):
-                tr = ps_t.tile([P, 4, P], F32, name="tr")
-                for g in range(2):
-                    turn2(tr, 2 * g, lambda u: src(i, g, u))
-                leave(
-                    dst.bitcast(F32)[:, 512 * i : 512 * i + 512].rearrange("p (g r u) -> p g r u", g=2, u=2),
-                    tr[:].rearrange("p (g u) r -> p g r u", u=2),
+                tr = turn([part(i, g, u) for g in range(2) for u in range(2)])
+                words = grp[kind, n][:].bitcast(F32)[:, HALF * i : HALF * i + HALF]
+                move(
+                    words.rearrange("p (g r u) -> p g r u", g=2, u=2),
+                    tr[:].rearrange("p (g u r) -> p g r u", g=2, u=2),
                     on[i],
                 )
 
-        def s_quant(src, n0, n1):
-            nc.vector.quantize_mx(
-                out=z2_q[:, n0:n1].rearrange("p n s g c -> p (n s g c)").bitcast(E5),
-                scales=z2_s[:, n0:n1].rearrange("p n s g c -> p (n s g c)"),
-                in_=src,
-            )
+        def rows_left(n, i):
+            return lambda k, g: row_codes[k][:, n, 256 * i + P * g : 256 * i + P * g + P]
 
         def zs(n):
             mask = mask_pool.tile([P, 2, U], BF16, name="mask")
-            nc.vector.tensor_scalar(out=mask[:], in0=z_sb[n][:], scalar1=0.0, scalar2=gain[:], op0=ALU.is_gt, op1=ALU.mult)
+            nc.vector.tensor_scalar(out=mask[:], in0=raw["z", n][:], scalar1=0.0, scalar2=gain[:], op0=ALU.is_gt, op1=ALU.mult)
             prod["mask", n] = mask
 
         def zm(n):
-            w_sb = mid.tile([P, 2, 2, HALF], BF16, name="w_sb")
-            sort_mult(w_sb[:], g_sb[n][:], prod["mask", n][:])
-            prod["z", n] = w_sb
+            prod["z", n] = sort_mult(raw["g", n][:], prod["mask", n][:])
 
-        def zt(n, on=("ACT", "ACT")):
-            grp["z", n] = mid.tile([P, 2048], BF16, align_bytes=64, name="gz")
-            s_turn(grp["z", n][:], lambda i, g, u: prod["z", n][:, u, i, 256 * g : 256 * g + 256], on)
+        def zt(n, on="SS"):
+            rows_turn("z", n, lambda i, g, u: prod["z", n][:, u, i, 256 * g : 256 * g + 256], on)
 
         def zq(n):
-            s_quant(grp["z", n][:], n, n + 1)
+            quantize(row_codes, n, grp["z", n], E5)
 
-        def p1(n, i, jh, on="ACT"):
-            acc = ps_m.tile([P, HALF], F32, name="acc")
-            mx(acc, [z2_q[:, n, i, g, :] for g in range(2)], [z2_s[:, n, i, g, :] for g in range(2)],
-               [w2_q[:, jh, g, :] for g in range(2)], [w2_s[:, jh, g, :] for g in range(2)], E5, E4)
-            leave(
-                dz1[n // 2][:, 2 * (n % 2) + i, HALF * jh : HALF * jh + HALF].rearrange("p (u q r) -> p u q r", u=2, q=16),
-                acc[:].rearrange("p (q u r) -> p u q r", u=2, q=16),
-                on,
-            )
+        def p1(n, jh, on="SS"):
+            for i in range(2):
+                acc = product(rows_left(n, i), E5, lambda k, g: w_codes[2][k][:, 2 * jh + g, :], E4)
+                move(
+                    dz1[n // 2, jh][:, 2 * (n % 2) + i, :].rearrange("p (u q r) -> p u q r", u=2, q=16),
+                    acc[:].rearrange("p (q u r) -> p u q r", u=2, q=16),
+                    on[i],
+                )
 
-        def tt(n, on=("ACT", "ACT")):
-            def part(i, g, u):
-                lo = HALF * g + 256 * u
-                return dz1[n // 2][:, 2 * (n % 2) + i, lo : lo + 256]
+        def tt(n, on="SS"):
+            rows_turn("t", n, lambda i, g, u: dz1[n // 2, g][:, 2 * (n % 2) + i, 256 * u : 256 * u + 256], on)
 
-            if ("t", n // 2) not in grp:
-                grp["t", n // 2] = new_grp(4096)
-            lo = 2048 * (n % 2)
-            s_turn(grp["t", n // 2][:, lo : lo + 2048], part, on)
+        def tq(n):
+            quantize(row_codes, n, grp["t", n], E5)
 
-        def tq(b):
-            s_quant(grp["t", b][:], 2 * b, 2 * b + 2)
-
-        def bl(b, jh, on="DVE"):
-            grp["b", b, jh] = mid.tile([P, 2048], BF16, align_bytes=64, name="grb")
-            src = dz1[b][:, :, HALF * jh : HALF * jh + HALF]
-            leave(
+        def bl(b, jh, on):
+            grp["b", b, jh] = new_group()
+            move(
                 grp["b", b, jh][:].rearrange("p (c i s) -> p c s i", s=4, i=4),
-                src.rearrange("p s (c i) -> p c s i", i=4),
+                dz1[b, jh][:].rearrange("p s (c i) -> p c s i", i=4),
                 on,
             )
 
         def bq(b, jh):
-            nc.vector.quantize_mx(out=db_q[:, b, jh, :].bitcast(E5), scales=db_s[:, b, jh, :], in_=grp["b", b, jh][:])
+            quantize(db_codes, 2 * jh + b, grp["b", b, jh], E5)
 
-        def hl(b, ih, on="DVE"):
-            if ("h", b) not in grp:
-                grp["h", b] = new_grp(4096)
-            dst = grp["h", b][:, 2048 * ih : 2048 * ih + 2048]
-            src = h_sb[b][:, :, HALF * ih : HALF * ih + HALF].rearrange("p s (c a) -> p a c s", a=4)
-            leave(dst.rearrange("p (a c s) -> p a c s", a=4, s=4), src, on)
-
-        def hq(b):
-            nc.vector.quantize_mx(
-                out=h_q[:, b].rearrange("p h c -> p (h c)").bitcast(E4),
-                scales=h_s[:, b].rearrange("p h c -> p (h c)"),
-                in_=grp["h", b][:],
+        def hl(b, ih, on):
+            grp["h", b, ih] = new_group()
+            move(
+                grp["h", b, ih][:].rearrange("p (a c s) -> p c s a", a=4, s=4),
+                raw["h", b][:, :, HALF * ih : HALF * ih + HALF].rearrange("p s (c a) -> p c s a", a=4),
+                on,
             )
 
-        def p3(it, jh, on="DVE"):
-            half, a = it // 4, it % 4
-            if ("res3", it) not in prod:
-                prod["res3", it] = raw4.tile([P, U], F32, name="r4")
-            res = prod["res3", it]
-            lo = P * a
-            acc = ps_m.tile([P, HALF], F32, name="acc")
-            mx(acc, [h_q[:, b, half, lo : lo + P] for b in range(2)], [h_s[:, b, half, lo : lo + P] for b in range(2)],
-               [db_q[:, b, jh, :] for b in range(2)], [db_s[:, b, jh, :] for b in range(2)], E4, E5)
+        def hq(b, ih):
+            quantize(h_codes, 2 * ih + b, grp["h", b, ih], E4)
+
+        def result(key):
+            if key not in res:
+                res[key] = big.tile([P, 2, U], F32, name="raw")
+            return res[key]
+
+        def p3(ih, a, jh):
+            acc = product(
+                lambda k, b: h_codes[k][:, 2 * ih + b, P * a : P * a + P], E4,
+                lambda k, b: db_codes[k][:, 2 * jh + b, :], E5,
+            )
             cols = slice(HALF * jh, HALF * jh + HALF)
-            unsorted = acc[:].rearrange("p (u q r) -> p q u r", u=2, q=16)
-            if on == "DVE":
-                nc.vector.tensor_tensor(
-                    out=res[:, cols].rearrange("p (q u r) -> p q u r", u=2, q=16),
-                    in0=unsorted,
-                    in1=m_sb[1, half][:, a, cols].rearrange("p (q u r) -> p q u r", u=2, q=16),
-                    op=ALU.mult,
-                )
-            else:
-                plain = plains.tile([P, HALF], F32, name="plain")
-                nc.scalar.copy(out=plain[:].rearrange("p (q u r) -> p q u r", u=2, q=16), in_=unsorted)
-                nc.gpsimd.tensor_tensor(out=res[:, cols], in0=plain[:], in1=m_sb[1, half][:, a, cols], op=ALU.mult)
+            nc.vector.tensor_tensor(
+                out=result((1, ih, a // 2))[:, a % 2, cols].rearrange("p (q u r) -> p q u r", u=2, q=16),
+                in0=acc[:].rearrange("p (u q r) -> p q u r", u=2, q=16),
+                in1=raw["m", 1, ih, a // 2][:, a % 2, cols].rearrange("p (q u r) -> p q u r", u=2, q=16),
+                op=ALU.mult,
+            )
 
-        def s3(it):
-            nc.sync.dma_start(out=out_1_v[it // 4][:, it % 4, :], in_=prod["res3", it][:])
+        def p2(ih, n, on="SS"):
+            for i in range(2):
+                acc = product(rows_left(n, i), E5, lambda k, g: w_codes[1][k][:, 2 * ih + g, :], E4)
+                move(result((0, n // 2, n % 2))[:, i, HALF * ih : HALF * ih + HALF], acc[:], on[i])
 
-        def p2(half, n, i, on="ACT"):
-            if ("res2", half, n) not in prod:
-                prod["res2", half, n] = raw4.tile([P, 2, HALF], F32, name="r4")
-            acc = ps_m.tile([P, HALF], F32, name="acc")
-            mx(acc, [z2_q[:, n, i, g, :] for g in range(2)], [z2_s[:, n, i, g, :] for g in range(2)],
-               [w1_q[:, half, g, :] for g in range(2)], [w1_s[:, half, g, :] for g in range(2)], E5, E4)
-            leave(prod["res2", half, n][:, i, :], acc[:], on)
+        def st(which, c, pair, slots=slice(0, 2), cols=slice(0, U)):
+            dst = (out_0_v, out_1_v)[which][c][:, 2 * pair : 2 * pair + 2, :]
+            nc.sync.dma_start(out=dst[:, slots, cols], in_=res[which, c, pair][:, slots, cols])
 
-        def s2(half, n):
-            b, s0 = n // 2, 2 * (n % 2)
-            nc.sync.dma_start(out=out_0_v[b][:, s0 : s0 + 2, HALF * half : HALF * half + HALF], in_=prod["res2", half, n][:])
-
-        def ld(kind, i):
-            if kind == "w":
-                if i == 0:
-                    for a in range(2):
-                        k_sb[2, 0, a] = load(raw4, "r4", [1, U], BF16, k2_v[0][:, a : a + 1, :])
-                        m_sb[2, 0, a] = load(raw4, "r4", [1, U], BF16, m2_v[0][:, a : a + 1, :])
-                else:
-                    k_sb[2, i] = load(raw4, "r4", [2, U], BF16, k2_v[i])
-                    m_sb[2, i] = load(raw4, "r4", [2, U], BF16, m2_v[i])
-            elif kind == "z":
-                b, s0 = i // 2, 2 * (i % 2)
-                z_sb[i] = load(raw8, "r8", [2, U], F32, z_v[b][:, s0 : s0 + 2, :])
-                g_sb[i] = load(raw4, "r4", [2, U], BF16, g_v[b][:, s0 : s0 + 2, :])
-            elif kind == "h":
-                h_sb[i] = load(raw_h, "hm", [4, U], BF16, h_v[i])
-            elif kind == "m":
-                m_sb[1, i] = load(raw_h, "hm", [4, U], BF16, m1_v[i])
-            else:
-                k_sb[1, i] = load(raw8, "r8", [4, U], BF16, k1_v[i])
-
-        ld("w", 2)
-        ld("z", 0)
-        ld("w", 0)
-        ld("w", 3)
-        ld("w", 1)
-        ld("z", 1)
-        ld("z", 3)
-        ld("z", 2)
-        ld("h", 0)
-        ld("m", 1)
-        ld("k", 1)
-        ld("k", 0)
-        ld("m", 0)
-        ld("h", 1)
         with tc.manual_schedule():
+            ld_w_pair(2,0,0)
+            ld_w_pair(2,0,1)
+            ld_z(0)
+            ld_z(1)
+            ld_w_pair(2,1,0)
+            ld_w_pair(2,1,1)
+            ld_z(2)
+            ld_z(3)
+            ld_w(1,0)
+            ld_w(1,1)
+            ld_h(0)
+            ld_h(1)
             nc.scalar.copy(out=gain_row[0:1, 0:1], in_=gain_in[0:1, :])
-            spread = ps_m.tile([P, HALF], F32, name="acc")
+            spread = bank()
             nc.tensor.matmul(spread[:, 0:64], lhsT=ones[:], rhs=gain_row[:], start=True, stop=True)
             nc.scalar.copy(out=gain[:], in_=spread[:, 0:1])
-            wm(2, 2)
+            wm(2,0,0)
+            wt(2,0,0)
+            wm(2,0,1)
+            wt(2,0,1)
             zs(0)
-            wt(2, 2, ("ACT", "ACT"))
             zm(0)
             zt(0)
-            wm(2, 0)
-            zq(0)
-            wm(2, 3)
-            wt(2, 0, ("DVE", "ACT"))
-            wt(2, 3)
-            wm(2, 1)
-            wt(2, 1)
-            wq(2, 1)
+            wq(2,0)
             zs(1)
-            p1(0, 1, 1)
+            zq(0)
             zm(1)
-            p1(0, 0, 1)
-            wq(2, 0)
-            zt(1)
-            p1(0, 0, 0)
-            zs(3)
+            p1(0,0)
+            wm(2,1,0)
+            zt(1,"SV")
+            wt(2,1,0)
+            wm(2,1,1)
             zq(1)
-            p1(0, 1, 0)
-            tt(0)
-            zm(3)
-            p1(1, 1, 1)
+            wt(2,1,1)
+            p1(1,0)
             zs(2)
+            wq(2,1)
             zm(2)
-            zt(3)
-            p1(1, 1, 0, "DVE")
-            p1(1, 0, 1)
-            p1(1, 0, 0)
-            zq(3)
+            p1(0,1)
             zt(2)
-            hl(0, 1)
-            bl(0, 0, "ACT")
-            hl(0, 0)
-            p1(3, 0, 0)
-            p1(3, 1, 1)
+            zs(3)
+            zm(3)
+            p1(1,1)
             zq(2)
-            hq(0)
-            p1(3, 1, 0)
-            wm(1, 1)
-            tt(1)
-            p1(2, 1, 1, "DVE")
-            p1(2, 0, 1, "DVE")
-            p1(3, 0, 1)
-            p1(2, 1, 0, "DVE")
+            zt(3)
+            bl(0,0,"V")
+            p1(2,0)
+            tt(0)
+            bq(0,0)
+            wm(1,0,0)
+            zq(3)
+            wm(1,0,1)
+            p1(2,1)
+            wt(1,0,0)
+            wt(1,0,1)
+            p1(3,0)
             tq(0)
-            p1(2, 0, 0)
-            wm(1, 0)
-            wt(1, 2)
-            wt(1, 3)
-            tt(2)
-            wq(1, 1)
-            tt(3, ("ACT", "DVE"))
-            hl(1, 0, "ACT")
-            wt(1, 1)
-            p2(1, 0, 0)
-            hl(1, 1)
-            p2(1, 0, 1)
+            bl(0,1,"V")
+            wm(1,1,0)
+            wm(1,1,1)
+            tt(1)
+            wq(1,0)
+            p1(3,1)
+            wt(1,1,0)
+            wt(1,1,1)
+            hl(0,0,"V")
             tq(1)
-            bl(1, 0)
-            wt(1, 0)
-            bq(0, 0)
-            p2(1, 1, 0, "DVE")
-            wq(1, 0)
-            bq(1, 0)
-            s2(1, 0)
-            p2(1, 1, 1)
-            p2(1, 3, 0)
-            p2(1, 3, 1)
-            hq(1)
-            bl(0, 1)
-            bl(1, 1)
-            p2(1, 2, 1)
-            s2(1, 1)
-            p2(1, 2, 0)
-            bq(0, 1)
-            p2(0, 3, 0)
-            p2(0, 3, 1)
-            s2(1, 3)
-            p2(0, 0, 0)
-            p2(0, 0, 1)
-            s2(1, 2)
-            p2(0, 1, 0)
-            p2(0, 1, 1)
-            bq(1, 1)
-            s2(0, 3)
-            s2(0, 0)
-            p2(0, 2, 1)
-            p2(0, 2, 0)
-            p3(4, 0)
-            p3(6, 0, "ACT")
-            p3(4, 1)
-            p3(6, 1)
-            s2(0, 1)
-            s2(0, 2)
-            p3(3, 1)
-            p3(2, 1, "ACT")
-            p3(3, 0)
-            p3(2, 0)
-            p3(7, 0)
-            p3(0, 1, "ACT")
-            s3(4)
-            s3(6)
-            p3(7, 1)
-            p3(0, 0)
-            p3(1, 1)
-            p3(1, 0)
-            s3(3)
-            p3(5, 0)
-            p3(5, 1)
-            s3(2)
-            s3(7)
-            s3(0)
-            s3(1)
-            s3(5)
+            bq(0,1)
+            p2(0,0)
+            st(0,0,0,slice(0,2),slice(0,HALF))
+            p2(0,1)
+            st(0,0,1,slice(0,2),slice(0,HALF))
+            bl(1,0,"V")
+            wq(1,1)
+            hl(1,0,"V")
+            tt(2)
+            tt(3)
+            p2(1,0)
+            st(0,0,0,slice(0,2),slice(HALF,U))
+            hq(0,0)
+            bq(1,0)
+            hq(1,0)
+            p2(1,1)
+            st(0,0,1,slice(0,2),slice(HALF,U))
+            tq(2)
+            tq(3)
+            bl(1,1,"V")
+            p3(0,0,0)
+            p3(0,1,0)
+            st(1,0,0,slice(0,2),slice(0,HALF))
+            hl(0,1,"S")
+            p3(0,2,0)
+            p3(0,3,0)
+            st(1,0,1,slice(0,2),slice(0,HALF))
+            bq(1,1)
+            hl(1,1,"V")
+            p2(0,2)
+            p2(1,2)
+            st(0,1,0)
+            p3(0,0,1)
+            p3(0,1,1)
+            st(1,0,0,slice(0,2),slice(HALF,U))
+            hq(0,1)
+            hq(1,1)
+            p2(0,3)
+            p3(0,2,1)
+            p3(0,3,1)
+            st(1,0,1,slice(0,2),slice(HALF,U))
+            p2(1,3)
+            st(0,1,1)
+            p3(1,0,0)
+            p3(1,0,1)
+            st(1,1,0,slice(0,1))
+            p3(1,1,0)
+            p3(1,1,1)
+            st(1,1,0,slice(1,2))
+            p3(1,2,0)
+            p3(1,2,1)
+            st(1,1,1,slice(0,1))
+            p3(1,3,0)
+            p3(1,3,1)
+            st(1,1,1,slice(1,2))

@@ -17,6 +17,7 @@ P = 128
 U = 1024
 HALF = 512
 GROUP = 2048
+GROUP_SLOTS = 6
 
 
 def tile_sparsefactorisationdense_pa_v_kernel(
@@ -38,7 +39,7 @@ def tile_sparsefactorisationdense_pa_v_kernel(
         small = ctx.enter_context(tc.tile_pool(name="small", bufs=10))
         mask_pool = ctx.enter_context(tc.tile_pool(name="mask_pool", bufs=2))
         prods = ctx.enter_context(tc.tile_pool(name="prods", bufs=3))
-        groups = ctx.enter_context(tc.tile_pool(name="groups", bufs=6))
+        groups = ctx.enter_context(tc.tile_pool(name="groups", bufs=1))
         keep = ctx.enter_context(tc.tile_pool(name="keep", bufs=1))
         psum = ctx.enter_context(tc.psum_pool(name="psum", bufs=8))
 
@@ -65,8 +66,11 @@ def tile_sparsefactorisationdense_pa_v_kernel(
         def bank():
             return psum.tile([P, HALF], F32, name="bank")
 
-        def new_group():
-            return groups.tile([P, GROUP], BF16, align_bytes=64, name="group")
+        raw, prod, grp, res, slot_of = {}, {}, {}, {}, {}
+
+        def new_group(key, behind=None):
+            slot_of[key] = len(slot_of) % GROUP_SLOTS if behind is None else slot_of[behind]
+            grp[key] = groups.tile([P, GROUP], BF16, align_bytes=64, name="group%d" % slot_of[key])
 
         def load(pool, slots, dtype, src):
             t = pool.tile([P, slots, U], dtype, name="raw")
@@ -112,7 +116,6 @@ def tile_sparsefactorisationdense_pa_v_kernel(
                 )
             return acc
 
-        raw, prod, grp, res = {}, {}, {}, {}
 
         def ld_w(f, half):
             raw_m = load(big, 4, BF16, m_v[f][half])
@@ -140,7 +143,7 @@ def tile_sparsefactorisationdense_pa_v_kernel(
             src = prod["w", f, half, pair]
             for g in range(2):
                 if pair == 0:
-                    grp["w", f, half, g] = new_group()
+                    new_group(("w", f, half, g))
                 tr = turn([src[:, u, a, 256 * g : 256 * g + 256] for a in range(2) for u in range(2)])
                 words = grp["w", f, half, g][:].bitcast(F32).rearrange("p (r a u) -> p r a u", a=4, u=2)
                 move(words[:, :, 2 * pair : 2 * pair + 2, :], tr[:].rearrange("p (a u r) -> p r a u", a=2, u=2), on[g])
@@ -150,7 +153,7 @@ def tile_sparsefactorisationdense_pa_v_kernel(
                 quantize(w_codes[f], 2 * half + g, grp["w", f, half, g], E4)
 
         def rows_turn(kind, n, part, on):
-            grp[kind, n] = new_group()
+            new_group((kind, n))
             for i in range(2):
                 tr = turn([part(i, g, u) for g in range(2) for u in range(2)])
                 words = grp[kind, n][:].bitcast(F32)[:, HALF * i : HALF * i + HALF]
@@ -193,7 +196,7 @@ def tile_sparsefactorisationdense_pa_v_kernel(
             quantize(row_codes, n, grp["t", n], E5)
 
         def bl(b, jh, on):
-            grp["b", b, jh] = new_group()
+            new_group(("b", b, jh))
             move(
                 grp["b", b, jh][:].rearrange("p (c i s) -> p c s i", s=4, i=4),
                 dz1[b, jh][:].rearrange("p s (c i) -> p c s i", i=4),
@@ -204,11 +207,22 @@ def tile_sparsefactorisationdense_pa_v_kernel(
             quantize(db_codes, 2 * jh + b, grp["b", b, jh], E5)
 
         def hl(b, ih, on):
-            grp["h", b, ih] = new_group()
+            new_group(("h", b, ih))
             move(
                 grp["h", b, ih][:].rearrange("p (a c s) -> p c s a", a=4, s=4),
                 raw["h", b][:, :, HALF * ih : HALF * ih + HALF].rearrange("p s (c a) -> p c s a", a=4),
                 on,
+            )
+
+        def hg(b, ih, behind):
+            new_group(("h", b, ih), behind)
+            nc.gpsimd.tensor_scalar(
+                out=grp["h", b, ih][:].rearrange("p (a c s) -> p a c s", a=4, s=4),
+                in0=raw["h", b][:, :, HALF * ih : HALF * ih + HALF].rearrange("p s (c a) -> p a c s", a=4),
+                scalar1=1.0,
+                scalar2=0.0,
+                op0=ALU.mult,
+                op1=ALU.add,
             )
 
         def hq(b, ih):
@@ -245,9 +259,9 @@ def tile_sparsefactorisationdense_pa_v_kernel(
             ld_w_pair(2,0,0)
             ld_w_pair(2,0,1)
             ld_z(0)
-            ld_z(1)
             ld_w_pair(2,1,0)
             ld_w_pair(2,1,1)
+            ld_z(1)
             ld_z(2)
             ld_z(3)
             ld_w(1,0)
@@ -266,92 +280,90 @@ def tile_sparsefactorisationdense_pa_v_kernel(
             zm(0)
             zt(0)
             wq(2,0)
-            zs(1)
-            zq(0)
-            zm(1)
-            p1(0,0)
             wm(2,1,0)
-            zt(1,"SV")
+            zq(0)
             wt(2,1,0)
             wm(2,1,1)
-            zq(1)
             wt(2,1,1)
-            p1(1,0)
-            zs(2)
+            p1(0,0)
+            zs(1)
+            zm(1)
             wq(2,1)
-            zm(2)
+            zt(1)
             p1(0,1)
+            zs(2)
+            zq(1)
+            zm(2)
+            tt(0)
+            p1(1,0)
             zt(2)
+            p1(1,1)
             zs(3)
             zm(3)
-            p1(1,1)
+            tq(0)
             zq(2)
             zt(3)
             bl(0,0,"V")
             p1(2,0)
-            tt(0)
-            bq(0,0)
-            wm(1,0,0)
             zq(3)
-            wm(1,0,1)
             p1(2,1)
+            wm(1,0,0)
+            wm(1,0,1)
+            tt(1)
+            p1(3,0)
             wt(1,0,0)
             wt(1,0,1)
-            p1(3,0)
-            tq(0)
-            bl(0,1,"V")
+            p1(3,1)
+            bq(0,0)
+            tq(1)
             wm(1,1,0)
             wm(1,1,1)
-            tt(1)
             wq(1,0)
-            p1(3,1)
+            tt(2)
             wt(1,1,0)
             wt(1,1,1)
-            hl(0,0,"V")
-            tq(1)
-            bq(0,1)
             p2(0,0)
             st(0,0,0,slice(0,2),slice(0,HALF))
+            bl(0,1,"V")
+            tq(2)
+            hl(0,0,"V")
             p2(0,1)
             st(0,0,1,slice(0,2),slice(0,HALF))
-            bl(1,0,"V")
             wq(1,1)
-            hl(1,0,"V")
-            tt(2)
             tt(3)
             p2(1,0)
             st(0,0,0,slice(0,2),slice(HALF,U))
+            bl(1,0,"V")
+            hl(1,0,"V")
             hq(0,0)
-            bq(1,0)
-            hq(1,0)
             p2(1,1)
             st(0,0,1,slice(0,2),slice(HALF,U))
-            tq(2)
-            tq(3)
-            bl(1,1,"V")
-            p3(0,0,0)
-            p3(0,1,0)
-            st(1,0,0,slice(0,2),slice(0,HALF))
-            hl(0,1,"S")
-            p3(0,2,0)
-            p3(0,3,0)
-            st(1,0,1,slice(0,2),slice(0,HALF))
-            bq(1,1)
-            hl(1,1,"V")
             p2(0,2)
             p2(1,2)
             st(0,1,0)
+            bq(1,0)
+            hq(1,0)
+            bl(1,1,"V")
+            tq(3)
+            bq(0,1)
+            bq(1,1)
+            hg(0,1,("b",1,1))
+            hl(1,1,"S")
+            p3(0,0,0)
+            p3(0,1,0)
+            p2(0,3)
             p3(0,0,1)
             p3(0,1,1)
-            st(1,0,0,slice(0,2),slice(HALF,U))
+            st(1,0,0)
             hq(0,1)
-            hq(1,1)
-            p2(0,3)
-            p3(0,2,1)
-            p3(0,3,1)
-            st(1,0,1,slice(0,2),slice(HALF,U))
             p2(1,3)
             st(0,1,1)
+            p3(0,2,0)
+            p3(0,3,0)
+            hq(1,1)
+            p3(0,2,1)
+            p3(0,3,1)
+            st(1,0,1)
             p3(1,0,0)
             p3(1,0,1)
             st(1,1,0,slice(0,1))
@@ -362,5 +374,6 @@ def tile_sparsefactorisationdense_pa_v_kernel(
             p3(1,2,1)
             st(1,1,1,slice(0,1))
             p3(1,3,0)
+            st(1,1,1,slice(1,2),slice(0,HALF))
             p3(1,3,1)
-            st(1,1,1,slice(1,2))
+            st(1,1,1,slice(1,2),slice(HALF,U))

@@ -68,8 +68,8 @@ def tile_sparsefactorisationdense_pa_v_kernel(
 
         raw, prod, grp, res, slot_of = {}, {}, {}, {}, {}
 
-        def new_group(key, behind=None):
-            slot_of[key] = len(slot_of) % GROUP_SLOTS if behind is None else slot_of[behind]
+        def new_group(key):
+            slot_of[key] = len(slot_of) % GROUP_SLOTS
             grp[key] = groups.tile([P, GROUP], BF16, align_bytes=64, name="group%d" % slot_of[key])
 
         def load(pool, slots, dtype, src):
@@ -214,17 +214,6 @@ def tile_sparsefactorisationdense_pa_v_kernel(
                 on,
             )
 
-        def hg(b, ih, behind):
-            new_group(("h", b, ih), behind)
-            nc.gpsimd.tensor_scalar(
-                out=grp["h", b, ih][:].rearrange("p (a c s) -> p a c s", a=4, s=4),
-                in0=raw["h", b][:, :, HALF * ih : HALF * ih + HALF].rearrange("p s (c a) -> p a c s", a=4),
-                scalar1=1.0,
-                scalar2=0.0,
-                op0=ALU.mult,
-                op1=ALU.add,
-            )
-
         def hq(b, ih):
             quantize(h_codes, 2 * ih + b, grp["h", b, ih], E4)
 
@@ -347,7 +336,6 @@ def tile_sparsefactorisationdense_pa_v_kernel(
             tq(3)
             bq(0,1)
             bq(1,1)
-            hg(0,1,("b",1,1))
             hl(1,1,"S")
             p3(0,0,0)
             p3(0,1,0)
@@ -355,15 +343,17 @@ def tile_sparsefactorisationdense_pa_v_kernel(
             p3(0,0,1)
             p3(0,1,1)
             st(1,0,0)
-            hq(0,1)
+            hl(0,1,"V")
             p2(1,3)
             st(0,1,1)
             p3(0,2,0)
-            p3(0,3,0)
+            hq(0,1)
             hq(1,1)
             p3(0,2,1)
+            st(1,0,1,slice(0,1))
+            p3(0,3,0)
             p3(0,3,1)
-            st(1,0,1)
+            st(1,0,1,slice(1,2))
             p3(1,0,0)
             p3(1,0,1)
             st(1,1,0,slice(0,1))

@@ -209,8 +209,8 @@ def tile_sparsefactorisationdense_pa_v_kernel(
         def hl(b, ih, on):
             new_group(("h", b, ih))
             move(
-                grp["h", b, ih][:].rearrange("p (a c s) -> p c s a", a=4, s=4),
-                raw["h", b][:, :, HALF * ih : HALF * ih + HALF].rearrange("p s (c a) -> p c s a", a=4),
+                grp["h", b, ih][:].rearrange("p (a c e s) -> p c s e a", a=4, e=2, s=4),
+                raw["h", b][:, :, HALF * ih : HALF * ih + HALF].rearrange("p s (c e a) -> p c s e a", e=2, a=4),
                 on,
             )
 

@@ -17,7 +17,6 @@ P = 128
 U = 1024
 HALF = 512
 GROUP = 2048
-GROUP_SLOTS = 6
 
 
 def tile_sparsefactorisationdense_pa_v_kernel(
@@ -35,11 +34,11 @@ def tile_sparsefactorisationdense_pa_v_kernel(
 
     with ExitStack() as ctx:
         const = ctx.enter_context(tc.tile_pool(name="const", bufs=1))
-        big = ctx.enter_context(tc.tile_pool(name="big", bufs=10))
-        small = ctx.enter_context(tc.tile_pool(name="small", bufs=10))
+        big = ctx.enter_context(tc.tile_pool(name="big", bufs=12))
+        small = ctx.enter_context(tc.tile_pool(name="small", bufs=6))
         mask_pool = ctx.enter_context(tc.tile_pool(name="mask_pool", bufs=2))
         prods = ctx.enter_context(tc.tile_pool(name="prods", bufs=3))
-        groups = ctx.enter_context(tc.tile_pool(name="groups", bufs=1))
+        groups = ctx.enter_context(tc.tile_pool(name="groups", bufs=7))
         keep = ctx.enter_context(tc.tile_pool(name="keep", bufs=1))
         psum = ctx.enter_context(tc.psum_pool(name="psum", bufs=8))
 
@@ -66,11 +65,10 @@ def tile_sparsefactorisationdense_pa_v_kernel(
         def bank():
             return psum.tile([P, HALF], F32, name="bank")
 
-        raw, prod, grp, res, slot_of = {}, {}, {}, {}, {}
+        raw, prod, grp, res = {}, {}, {}, {}
 
         def new_group(key):
-            slot_of[key] = len(slot_of) % GROUP_SLOTS
-            grp[key] = groups.tile([P, GROUP], BF16, align_bytes=64, name="group%d" % slot_of[key])
+            grp[key] = groups.tile([P, GROUP], BF16, align_bytes=64, name="group")
 
         def load(pool, slots, dtype, src):
             t = pool.tile([P, slots, U], dtype, name="raw")
@@ -245,8 +243,7 @@ def tile_sparsefactorisationdense_pa_v_kernel(
             nc.sync.dma_start(out=dst[:, slots, cols], in_=res[which, c, pair][:, slots, cols])
 
         with tc.manual_schedule():
-            ld_w_pair(2,0,0)
-            ld_w_pair(2,0,1)
+            ld_w(2,0)
             ld_z(0)
             ld_w_pair(2,1,0)
             ld_w_pair(2,1,1)
@@ -289,9 +286,9 @@ def tile_sparsefactorisationdense_pa_v_kernel(
             p1(1,1)
             zs(3)
             zm(3)
-            tq(0)
             zq(2)
             zt(3)
+            tq(0)
             bl(0,0,"V")
             p1(2,0)
             zq(3)
@@ -302,18 +299,18 @@ def tile_sparsefactorisationdense_pa_v_kernel(
             p1(3,0)
             wt(1,0,0)
             wt(1,0,1)
-            p1(3,1)
             bq(0,0)
             tq(1)
+            bl(0,1,"V")
             wm(1,1,0)
             wm(1,1,1)
             wq(1,0)
             tt(2)
+            p1(3,1)
             wt(1,1,0)
             wt(1,1,1)
             p2(0,0)
             st(0,0,0,slice(0,2),slice(0,HALF))
-            bl(0,1,"V")
             tq(2)
             hl(0,0,"V")
             p2(0,1)

@@ -34,8 +34,8 @@ def tile_sparsefactorisationdense_pa_v_kernel(
 
     with ExitStack() as ctx:
         const = ctx.enter_context(tc.tile_pool(name="const", bufs=1))
-        big = ctx.enter_context(tc.tile_pool(name="big", bufs=12))
-        small = ctx.enter_context(tc.tile_pool(name="small", bufs=6))
+        big = ctx.enter_context(tc.tile_pool(name="big", bufs=13))
+        small = ctx.enter_context(tc.tile_pool(name="small", bufs=4))
         mask_pool = ctx.enter_context(tc.tile_pool(name="mask_pool", bufs=2))
         prods = ctx.enter_context(tc.tile_pool(name="prods", bufs=3))
         groups = ctx.enter_context(tc.tile_pool(name="groups", bufs=7))
@@ -245,8 +245,7 @@ def tile_sparsefactorisationdense_pa_v_kernel(
         with tc.manual_schedule():
             ld_w(2,0)
             ld_z(0)
-            ld_w_pair(2,1,0)
-            ld_w_pair(2,1,1)
+            ld_w(2,1)
             ld_z(1)
             ld_z(2)
             ld_z(3)
@@ -266,10 +265,10 @@ def tile_sparsefactorisationdense_pa_v_kernel(
             zm(0)
             zt(0)
             wq(2,0)
-            wm(2,1,0)
             zq(0)
-            wt(2,1,0)
+            wm(2,1,0)
             wm(2,1,1)
+            wt(2,1,0)
             wt(2,1,1)
             p1(0,0)
             zs(1)
@@ -347,20 +346,17 @@ def tile_sparsefactorisationdense_pa_v_kernel(
             hq(0,1)
             hq(1,1)
             p3(0,2,1)
-            st(1,0,1,slice(0,1))
             p3(0,3,0)
             p3(0,3,1)
-            st(1,0,1,slice(1,2))
+            st(1,0,1)
             p3(1,0,0)
             p3(1,0,1)
-            st(1,1,0,slice(0,1))
             p3(1,1,0)
             p3(1,1,1)
-            st(1,1,0,slice(1,2))
+            st(1,1,0)
             p3(1,2,0)
             p3(1,2,1)
             st(1,1,1,slice(0,1))
             p3(1,3,0)
-            st(1,1,1,slice(1,2),slice(0,HALF))
             p3(1,3,1)
-            st(1,1,1,slice(1,2),slice(HALF,U))
+            st(1,1,1,slice(1,2))

@@ -238,9 +238,9 @@ def tile_sparsefactorisationdense_pa_v_kernel(
                 acc = product(rows_left(n, i), E5, lambda k, g: w_codes[1][k][:, 2 * ih + g, :], E4)
                 move(result((0, n // 2, n % 2))[:, i, HALF * ih : HALF * ih + HALF], acc[:], on[i])
 
-        def st(which, c, pair, slots=slice(0, 2), cols=slice(0, U)):
+        def st(which, c, pair, slots=slice(0, 2), cols=slice(0, U), queue=nc.sync):
             dst = (out_0_v, out_1_v)[which][c][:, 2 * pair : 2 * pair + 2, :]
-            nc.sync.dma_start(out=dst[:, slots, cols], in_=res[which, c, pair][:, slots, cols])
+            queue.dma_start(out=dst[:, slots, cols], in_=res[which, c, pair][:, slots, cols])
 
         with tc.manual_schedule():
             ld_w(2,0)
@@ -348,7 +348,7 @@ def tile_sparsefactorisationdense_pa_v_kernel(
             p3(0,2,1)
             p3(0,3,0)
             p3(0,3,1)
-            st(1,0,1)
+            st(1,0,1,queue=nc.scalar)
             p3(1,0,0)
             p3(1,0,1)
             p3(1,1,0)
@@ -356,7 +356,7 @@ def tile_sparsefactorisationdense_pa_v_kernel(
             st(1,1,0)
             p3(1,2,0)
             p3(1,2,1)
-            st(1,1,1,slice(0,1))
+            st(1,1,1,slice(0,1),queue=nc.scalar)
             p3(1,3,0)
             p3(1,3,1)
             st(1,1,1,slice(1,2))

@@ -17,6 +17,7 @@ P = 128
 U = 1024
 HALF = 512
 GROUP = 2048
+DMA_ALIGN = 256
 
 
 def tile_sparsefactorisationdense_pa_v_kernel(
@@ -71,7 +72,7 @@ def tile_sparsefactorisationdense_pa_v_kernel(
             grp[key] = groups.tile([P, GROUP], BF16, align_bytes=64, name="group")
 
         def load(pool, slots, dtype, src):
-            t = pool.tile([P, slots, U], dtype, name="raw")
+            t = pool.tile([P, slots, U], dtype, align_bytes=DMA_ALIGN, name="raw")
             nc.sync.dma_start(out=t[:], in_=src)
             return t
 
@@ -217,7 +218,7 @@ def tile_sparsefactorisationdense_pa_v_kernel(
 
         def result(key):
             if key not in res:
-                res[key] = big.tile([P, 2, U], F32, name="raw")
+                res[key] = big.tile([P, 2, U], F32, align_bytes=DMA_ALIGN, name="raw")
             return res[key]
 
         def p3(ih, a, jh):

@@ -69,10 +69,10 @@ def tile_sparsefactorisationdense_pa_v_kernel(
         raw, prod, grp, res = {}, {}, {}, {}
 
         def new_group(key):
-            grp[key] = groups.tile([P, GROUP], BF16, align_bytes=64, name="group")
+            grp[key] = groups.tile([P, GROUP], BF16, align_bytes=64, tag="group", name="g_" + "".join(str(x) for x in key))
 
-        def load(pool, slots, dtype, src):
-            t = pool.tile([P, slots, U], dtype, align_bytes=DMA_ALIGN, name="raw")
+        def load(pool, slots, dtype, src, name="raw"):
+            t = pool.tile([P, slots, U], dtype, align_bytes=DMA_ALIGN, tag="raw", name=name)
             nc.sync.dma_start(out=t[:], in_=src)
             return t
 
@@ -117,8 +117,8 @@ def tile_sparsefactorisationdense_pa_v_kernel(
 
 
         def ld_w(f, half):
-            raw_m = load(big, 4, BF16, m_v[f][half])
-            raw_k = load(big, 4, BF16, k_v[f][half])
+            raw_m = load(big, 4, BF16, m_v[f][half], "m%d%d" % (f, half))
+            raw_k = load(big, 4, BF16, k_v[f][half], "k%d%d" % (f, half))
             for pair in range(2):
                 raw["m", f, half, pair] = raw_m[:, 2 * pair : 2 * pair + 2, :]
                 raw["k", f, half, pair] = raw_k[:, 2 * pair : 2 * pair + 2, :]
@@ -129,11 +129,11 @@ def tile_sparsefactorisationdense_pa_v_kernel(
 
         def ld_z(n):
             lo = 2 * (n % 2)
-            raw["z", n] = load(big, 2, F32, z_v[n // 2][:, lo : lo + 2, :])
-            raw["g", n] = load(small, 2, BF16, g_v[n // 2][:, lo : lo + 2, :])
+            raw["z", n] = load(big, 2, F32, z_v[n // 2][:, lo : lo + 2, :], "z%d" % n)
+            raw["g", n] = load(small, 2, BF16, g_v[n // 2][:, lo : lo + 2, :], "g%d" % n)
 
         def ld_h(b):
-            raw["h", b] = load(big, 4, BF16, h_v[b])
+            raw["h", b] = load(big, 4, BF16, h_v[b], "h%d" % b)
 
         def wm(f, half, pair):
             prod["w", f, half, pair] = sort_mult(raw["k", f, half, pair], raw["m", f, half, pair])
@@ -147,8 +147,8 @@ def tile_sparsefactorisationdense_pa_v_kernel(
                 words = grp["w", f, half, g][:].bitcast(F32).rearrange("p (r a u) -> p r a u", a=4, u=2)
                 move(words[:, :, 2 * pair : 2 * pair + 2, :], tr[:].rearrange("p (a u r) -> p r a u", a=2, u=2), on[g])
 
-        def wq(f, half):
-            for g in range(2):
+        def wq(f, half, gs=(0, 1)):
+            for g in gs:
                 quantize(w_codes[f], 2 * half + g, grp["w", f, half, g], E4)
 
         def rows_turn(kind, n, part, on):
@@ -179,8 +179,8 @@ def tile_sparsefactorisationdense_pa_v_kernel(
         def zq(n):
             quantize(row_codes, n, grp["z", n], E5)
 
-        def p1(n, jh, on="SS"):
-            for i in range(2):
+        def p1(n, jh, on="SS", tiles=(0, 1)):
+            for i in tiles:
                 acc = product(rows_left(n, i), E5, lambda k, g: w_codes[2][k][:, 2 * jh + g, :], E4)
                 move(
                     dz1[n // 2, jh][:, 2 * (n % 2) + i, :].rearrange("p (u q r) -> p u q r", u=2, q=16),
@@ -218,7 +218,7 @@ def tile_sparsefactorisationdense_pa_v_kernel(
 
         def result(key):
             if key not in res:
-                res[key] = big.tile([P, 2, U], F32, align_bytes=DMA_ALIGN, name="raw")
+                res[key] = big.tile([P, 2, U], F32, align_bytes=DMA_ALIGN, tag="raw", name="r" + "".join(str(x) for x in key))
             return res[key]
 
         def p3(ih, a, jh):
@@ -234,14 +234,20 @@ def tile_sparsefactorisationdense_pa_v_kernel(
                 op=ALU.mult,
             )
 
-        def p2(ih, n, on="SS"):
-            for i in range(2):
+        def p2(ih, n, on="SS", tiles=(0, 1)):
+            for i in tiles:
                 acc = product(rows_left(n, i), E5, lambda k, g: w_codes[1][k][:, 2 * ih + g, :], E4)
                 move(result((0, n // 2, n % 2))[:, i, HALF * ih : HALF * ih + HALF], acc[:], on[i])
 
         def st(which, c, pair, slots=slice(0, 2), cols=slice(0, U), queue=nc.sync):
             dst = (out_0_v, out_1_v)[which][c][:, 2 * pair : 2 * pair + 2, :]
             queue.dma_start(out=dst[:, slots, cols], in_=res[which, c, pair][:, slots, cols])
+
+        def spread_gain():
+            nc.scalar.copy(out=gain_row[0:1, 0:1], in_=gain_in[0:1, :])
+            spread = bank()
+            nc.tensor.matmul(spread[:, 0:64], lhsT=ones[:], rhs=gain_row[:], start=True, stop=True)
+            nc.scalar.copy(out=gain[:], in_=spread[:, 0:1])
 
         with tc.manual_schedule():
             ld_w(2,0)
@@ -254,10 +260,7 @@ def tile_sparsefactorisationdense_pa_v_kernel(
             ld_w(1,1)
             ld_h(0)
             ld_h(1)
-            nc.scalar.copy(out=gain_row[0:1, 0:1], in_=gain_in[0:1, :])
-            spread = bank()
-            nc.tensor.matmul(spread[:, 0:64], lhsT=ones[:], rhs=gain_row[:], start=True, stop=True)
-            nc.scalar.copy(out=gain[:], in_=spread[:, 0:1])
+            spread_gain()
             wm(2,0,0)
             wt(2,0,0)
             wm(2,0,1)
@@ -285,11 +288,12 @@ def tile_sparsefactorisationdense_pa_v_kernel(
             zt(2)
             p1(1,1)
             zs(3)
+            tq(0)
             zm(3)
             zq(2)
             zt(3)
-            tq(0)
             bl(0,0,"V")
+            bl(0,1,"V")
             p1(2,0)
             zq(3)
             p1(2,1)
@@ -301,14 +305,14 @@ def tile_sparsefactorisationdense_pa_v_kernel(
             wt(1,0,1)
             bq(0,0)
             tq(1)
-            bl(0,1,"V")
+            bq(0,1)
             wm(1,1,0)
             wm(1,1,1)
             wq(1,0)
             tt(2)
             p1(3,1)
             wt(1,1,0)
-            wt(1,1,1)
+            wt(1,1,1,"VS")
             p2(0,0)
             st(0,0,0,slice(0,2),slice(0,HALF))
             tq(2)
@@ -321,43 +325,51 @@ def tile_sparsefactorisationdense_pa_v_kernel(
             st(0,0,0,slice(0,2),slice(HALF,U))
             bl(1,0,"V")
             hl(1,0,"V")
+            tq(3)
             hq(0,0)
             p2(1,1)
             st(0,0,1,slice(0,2),slice(HALF,U))
-            p2(0,2)
-            p2(1,2)
-            st(0,1,0)
+            p2(0,2,tiles=(0,))
+            p2(1,2,tiles=(0,))
+            st(0,1,0,slice(0,1))
+            p2(0,2,tiles=(1,))
+            p2(1,2,tiles=(1,))
+            st(0,1,0,slice(1,2))
             bq(1,0)
-            hq(1,0)
             bl(1,1,"V")
-            tq(3)
-            bq(0,1)
+            hq(1,0)
             bq(1,1)
+            p2(0,3,tiles=(0,))
+            p2(1,3,tiles=(0,))
+            st(0,1,1,slice(0,1))
+            p2(0,3,tiles=(1,))
+            p2(1,3,tiles=(1,))
+            st(0,1,1,slice(1,2))
             hl(1,1,"S")
-            p3(0,0,0)
-            p3(0,1,0)
-            p2(0,3)
-            p3(0,0,1)
-            p3(0,1,1)
-            st(1,0,0)
             hl(0,1,"V")
-            p2(1,3)
-            st(0,1,1)
-            p3(0,2,0)
+            p3(0,0,0)
+            p3(0,0,1)
+            st(1,0,0,slice(0,1))
+            p3(0,1,0)
+            p3(0,1,1)
+            st(1,0,0,slice(1,2))
             hq(0,1)
-            hq(1,1)
+            p3(0,2,0)
             p3(0,2,1)
+            st(1,0,1,slice(0,1))
+            hq(1,1)
             p3(0,3,0)
             p3(0,3,1)
-            st(1,0,1,queue=nc.scalar)
+            st(1,0,1,slice(1,2),queue=nc.scalar)
             p3(1,0,0)
             p3(1,0,1)
+            st(1,1,0,slice(0,1))
             p3(1,1,0)
             p3(1,1,1)
-            st(1,1,0)
+            st(1,1,0,slice(1,2),queue=nc.scalar)
             p3(1,2,0)
             p3(1,2,1)
-            st(1,1,1,slice(0,1),queue=nc.scalar)
+            st(1,1,1,slice(0,1))
             p3(1,3,0)
             p3(1,3,1)
-            st(1,1,1,slice(1,2))
+            st(1,1,1,slice(1,2),queue=nc.scalar)

@@ -17,7 +17,7 @@ P = 128
 U = 1024
 HALF = 512
 GROUP = 2048
-DMA_ALIGN = 256
+DMA_ALIGN = 2048
 
 
 def tile_sparsefactorisationdense_pa_v_kernel(
@@ -28,10 +28,13 @@ def tile_sparsefactorisationdense_pa_v_kernel(
     def by_slots(x):
         return x.rearrange("(c p s) w -> c p s w", p=P, s=4)
 
-    k_v = {1: by_slots(k1), 2: by_slots(k2)}
-    m_v = {1: by_slots(m1), 2: by_slots(m2)}
+    def by_tiles(x):
+        return x.rearrange("(c a p) w -> c p a w", p=P, a=4)
+
+    k_v = {1: by_tiles(k1), 2: by_slots(k2)}
+    m_v = {1: by_tiles(m1), 2: by_slots(m2)}
     z_v, g_v, h_v = by_slots(z), by_slots(grad_out), by_slots(h0)
-    out_0_v, out_1_v = by_slots(out_0), by_slots(out_1)
+    out_0_v, out_1_v = by_slots(out_0), by_tiles(out_1)
 
     with ExitStack() as ctx:
         const = ctx.enter_context(tc.tile_pool(name="const", bufs=1))
@@ -132,6 +135,15 @@ def tile_sparsefactorisationdense_pa_v_kernel(
             raw["z", n] = load(big, 2, F32, z_v[n // 2][:, lo : lo + 2, :], "z%d" % n)
             raw["g", n] = load(small, 2, BF16, g_v[n // 2][:, lo : lo + 2, :], "g%d" % n)
 
+        def ld_zz(n):
+            lo = 2 * (n % 2)
+            raw["z", n] = load(big, 2, F32, z_v[n // 2][:, lo : lo + 2, :], "z%d" % n)
+
+        def ld_g(b):
+            both = load(big, 4, BF16, g_v[b], "g%d" % b)
+            for i in range(2):
+                raw["g", 2 * b + i] = both[:, 2 * i : 2 * i + 2, :]
+
         def ld_h(b):
             raw["h", b] = load(big, 4, BF16, h_v[b], "h%d" % b)
 
@@ -144,8 +156,13 @@ def tile_sparsefactorisationdense_pa_v_kernel(
                 if pair == 0:
                     new_group(("w", f, half, g))
                 tr = turn([src[:, u, a, 256 * g : 256 * g + 256] for a in range(2) for u in range(2)])
-                words = grp["w", f, half, g][:].bitcast(F32).rearrange("p (r a u) -> p r a u", a=4, u=2)
-                move(words[:, :, 2 * pair : 2 * pair + 2, :], tr[:].rearrange("p (a u r) -> p r a u", a=2, u=2), on[g])
+                words = grp["w", f, half, g][:].bitcast(F32)
+                if f == 2:
+                    words = words.rearrange("p (r a u) -> p r a u", a=4, u=2)[:, :, 2 * pair : 2 * pair + 2, :]
+                    move(words, tr[:].rearrange("p (a u r) -> p r a u", a=2, u=2), on[g])
+                else:
+                    words = words[:, HALF * pair : HALF * pair + HALF].rearrange("p (a r u) -> p a r u", a=2, u=2)
+                    move(words, tr[:].rearrange("p (a u r) -> p a r u", a=2, u=2), on[g])
 
         def wq(f, half, gs=(0, 1)):
             for g in gs:
@@ -205,16 +222,22 @@ def tile_sparsefactorisationdense_pa_v_kernel(
         def bq(b, jh):
             quantize(db_codes, 2 * jh + b, grp["b", b, jh], E5)
 
-        def hl(b, ih, on):
-            new_group(("h", b, ih))
-            move(
-                grp["h", b, ih][:].rearrange("p (a c e s) -> p c s e a", a=4, e=2, s=4),
-                raw["h", b][:, :, HALF * ih : HALF * ih + HALF].rearrange("p s (c e a) -> p c s e a", e=2, a=4),
-                on,
-            )
+        def hl(ih, ah, b, on):
+            if ("h", ih, ah) not in grp:
+                new_group(("h", ih, ah))
+            dst = grp["h", ih, ah][:, U * b : U * b + U]
+            lo = HALF * ih + 256 * ah
+            src = raw["h", b][:, :, lo : lo + 256]
+            if on == "V":
+                nc.vector.tensor_copy(
+                    out=dst.rearrange("p (c i s) -> p c s i", i=4, s=4),
+                    in_=src.rearrange("p s (c i) -> p c s i", i=4),
+                )
+            else:
+                nc.scalar.copy(out=dst.rearrange("p (c s) -> p c s", s=4), in_=src.rearrange("p s c -> p c s"))
 
-        def hq(b, ih):
-            quantize(h_codes, 2 * ih + b, grp["h", b, ih], E4)
+        def hq(ih, ah):
+            quantize(h_codes, 2 * ih + ah, grp["h", ih, ah], E4)
 
         def result(key):
             if key not in res:
@@ -223,7 +246,7 @@ def tile_sparsefactorisationdense_pa_v_kernel(
 
         def p3(ih, a, jh):
             acc = product(
-                lambda k, b: h_codes[k][:, 2 * ih + b, P * a : P * a + P], E4,
+                lambda k, b: h_codes[k][:, 2 * ih + a // 2, 256 * b + P * (a % 2) : 256 * b + P * (a % 2) + P], E4,
                 lambda k, b: db_codes[k][:, 2 * jh + b, :], E5,
             )
             cols = slice(HALF * jh, HALF * jh + HALF)
@@ -316,28 +339,28 @@ def tile_sparsefactorisationdense_pa_v_kernel(
             p2(0,0)
             st(0,0,0,slice(0,2),slice(0,HALF))
             tq(2)
-            hl(0,0,"V")
+            hl(0,0,0,"V")
+            hl(0,1,0,"V")
+            wq(1,1)
             p2(0,1)
             st(0,0,1,slice(0,2),slice(0,HALF))
-            wq(1,1)
-            tt(3)
+            p2(0,2)
+            st(0,1,0,slice(0,2),slice(0,HALF))
+            bl(1,0,"V")
+            tt(3,"VS")
             p2(1,0)
             st(0,0,0,slice(0,2),slice(HALF,U))
-            bl(1,0,"V")
-            hl(1,0,"V")
+            hl(0,0,1,"V")
+            hl(0,1,1,"V")
             tq(3)
             hq(0,0)
-            p2(1,1)
-            st(0,0,1,slice(0,2),slice(HALF,U))
-            p2(0,2,tiles=(0,))
-            p2(1,2,tiles=(0,))
-            st(0,1,0,slice(0,1))
-            p2(0,2,tiles=(1,))
-            p2(1,2,tiles=(1,))
-            st(0,1,0,slice(1,2))
             bq(1,0)
             bl(1,1,"V")
-            hq(1,0)
+            p2(1,1)
+            st(0,0,1,slice(0,2),slice(HALF,U))
+            p2(1,2)
+            st(0,1,0,slice(0,2),slice(HALF,U))
+            hq(0,1)
             bq(1,1)
             p2(0,3,tiles=(0,))
             p2(1,3,tiles=(0,))
@@ -345,25 +368,27 @@ def tile_sparsefactorisationdense_pa_v_kernel(
             p2(0,3,tiles=(1,))
             p2(1,3,tiles=(1,))
             st(0,1,1,slice(1,2))
-            hl(1,1,"S")
-            hl(0,1,"V")
+            hl(1,0,0,"S")
+            hl(1,0,1,"S")
+            hl(1,1,0,"S")
+            hl(1,1,1,"S")
             p3(0,0,0)
             p3(0,0,1)
             st(1,0,0,slice(0,1))
             p3(0,1,0)
             p3(0,1,1)
             st(1,0,0,slice(1,2))
-            hq(0,1)
             p3(0,2,0)
             p3(0,2,1)
             st(1,0,1,slice(0,1))
-            hq(1,1)
+            hq(1,0)
             p3(0,3,0)
             p3(0,3,1)
-            st(1,0,1,slice(1,2),queue=nc.scalar)
+            st(1,0,1,slice(1,2))
             p3(1,0,0)
             p3(1,0,1)
             st(1,1,0,slice(0,1))
+            hq(1,1)
             p3(1,1,0)
             p3(1,1,1)
             st(1,1,0,slice(1,2),queue=nc.scalar)

@@ -28,13 +28,13 @@ def tile_sparsefactorisationdense_pa_v_kernel(
     def by_slots(x):
         return x.rearrange("(c p s) w -> c p s w", p=P, s=4)
 
-    def by_tiles(x):
-        return x.rearrange("(c a p) w -> c p a w", p=P, a=4)
+    def by_pairs(x):
+        return x.rearrange("(c a p e) w -> c p a e w", p=P, a=2, e=2)
 
-    k_v = {1: by_tiles(k1), 2: by_slots(k2)}
-    m_v = {1: by_tiles(m1), 2: by_slots(m2)}
+    k_v = {1: by_pairs(k1), 2: by_slots(k2)}
+    m_v = {1: by_pairs(m1), 2: by_slots(m2)}
     z_v, g_v, h_v = by_slots(z), by_slots(grad_out), by_slots(h0)
-    out_0_v, out_1_v = by_slots(out_0), by_tiles(out_1)
+    out_0_v, out_1_v = by_slots(out_0), by_pairs(out_1)
 
     with ExitStack() as ctx:
         const = ctx.enter_context(tc.tile_pool(name="const", bufs=1))
@@ -76,7 +76,7 @@ def tile_sparsefactorisationdense_pa_v_kernel(
 
         def load(pool, slots, dtype, src, name="raw"):
             t = pool.tile([P, slots, U], dtype, align_bytes=DMA_ALIGN, tag="raw", name=name)
-            nc.sync.dma_start(out=t[:], in_=src)
+            nc.sync.dma_start(out=t[:] if len(src.shape) == 3 else t[:].rearrange("p (a e) w -> p a e w", e=2), in_=src)
             return t
 
         def sort_mult(a, b):
@@ -150,10 +150,10 @@ def tile_sparsefactorisationdense_pa_v_kernel(
         def wm(f, half, pair):
             prod["w", f, half, pair] = sort_mult(raw["k", f, half, pair], raw["m", f, half, pair])
 
-        def wt(f, half, pair, on="SS"):
+        def wt(f, half, pair, on="SS", gs=(0, 1)):
             src = prod["w", f, half, pair]
-            for g in range(2):
-                if pair == 0:
+            for g in gs:
+                if ("w", f, half, g) not in grp:
                     new_group(("w", f, half, g))
                 tr = turn([src[:, u, a, 256 * g : 256 * g + 256] for a in range(2) for u in range(2)])
                 words = grp["w", f, half, g][:].bitcast(F32)
@@ -161,16 +161,17 @@ def tile_sparsefactorisationdense_pa_v_kernel(
                     words = words.rearrange("p (r a u) -> p r a u", a=4, u=2)[:, :, 2 * pair : 2 * pair + 2, :]
                     move(words, tr[:].rearrange("p (a u r) -> p r a u", a=2, u=2), on[g])
                 else:
-                    words = words[:, HALF * pair : HALF * pair + HALF].rearrange("p (a r u) -> p a r u", a=2, u=2)
-                    move(words, tr[:].rearrange("p (a u r) -> p a r u", a=2, u=2), on[g])
+                    words = words[:, HALF * pair : HALF * pair + HALF].rearrange("p (r a u) -> p r a u", a=2, u=2)
+                    move(words, tr[:].rearrange("p (a u r) -> p r a u", a=2, u=2), on[g])
 
         def wq(f, half, gs=(0, 1)):
             for g in gs:
                 quantize(w_codes[f], 2 * half + g, grp["w", f, half, g], E4)
 
-        def rows_turn(kind, n, part, on):
-            new_group((kind, n))
-            for i in range(2):
+        def rows_turn(kind, n, part, on, tiles):
+            if (kind, n) not in grp:
+                new_group((kind, n))
+            for i in tiles:
                 tr = turn([part(i, g, u) for g in range(2) for u in range(2)])
                 words = grp[kind, n][:].bitcast(F32)[:, HALF * i : HALF * i + HALF]
                 move(
@@ -190,8 +191,8 @@ def tile_sparsefactorisationdense_pa_v_kernel(
         def zm(n):
             prod["z", n] = sort_mult(raw["g", n][:], prod["mask", n][:])
 
-        def zt(n, on="SS"):
-            rows_turn("z", n, lambda i, g, u: prod["z", n][:, u, i, 256 * g : 256 * g + 256], on)
+        def zt(n, on="SS", tiles=(0, 1)):
+            rows_turn("z", n, lambda i, g, u: prod["z", n][:, u, i, 256 * g : 256 * g + 256], on, tiles)
 
         def zq(n):
             quantize(row_codes, n, grp["z", n], E5)
@@ -205,8 +206,8 @@ def tile_sparsefactorisationdense_pa_v_kernel(
                     on[i],
                 )
 
-        def tt(n, on="SS"):
-            rows_turn("t", n, lambda i, g, u: dz1[n // 2, g][:, 2 * (n % 2) + i, 256 * u : 256 * u + 256], on)
+        def tt(n, on="SS", tiles=(0, 1)):
+            rows_turn("t", n, lambda i, g, u: dz1[n // 2, g][:, 2 * (n % 2) + i, 256 * u : 256 * u + 256], on, tiles)
 
         def tq(n):
             quantize(row_codes, n, grp["t", n], E5)
@@ -228,13 +229,11 @@ def tile_sparsefactorisationdense_pa_v_kernel(
             dst = grp["h", ih, ah][:, U * b : U * b + U]
             lo = HALF * ih + 256 * ah
             src = raw["h", b][:, :, lo : lo + 256]
-            if on == "V":
-                nc.vector.tensor_copy(
-                    out=dst.rearrange("p (c i s) -> p c s i", i=4, s=4),
-                    in_=src.rearrange("p s (c i) -> p c s i", i=4),
-                )
-            else:
-                nc.scalar.copy(out=dst.rearrange("p (c s) -> p c s", s=4), in_=src.rearrange("p s c -> p c s"))
+            move(
+                dst.rearrange("p (e c i s) -> p c s i e", e=2, i=2, s=4),
+                src.rearrange("p s (c i e) -> p c s i e", i=2, e=2),
+                on,
+            )
 
         def hq(ih, ah):
             quantize(h_codes, 2 * ih + ah, grp["h", ih, ah], E4)
@@ -263,7 +262,7 @@ def tile_sparsefactorisationdense_pa_v_kernel(
                 move(result((0, n // 2, n % 2))[:, i, HALF * ih : HALF * ih + HALF], acc[:], on[i])
 
         def st(which, c, pair, slots=slice(0, 2), cols=slice(0, U), queue=nc.sync):
-            dst = (out_0_v, out_1_v)[which][c][:, 2 * pair : 2 * pair + 2, :]
+            dst = out_1_v[c][:, pair] if which else out_0_v[c][:, 2 * pair : 2 * pair + 2, :]
             queue.dma_start(out=dst[:, slots, cols], in_=res[which, c, pair][:, slots, cols])
 
         def spread_gain():

from contextlib import ExitStack

import concourse.mybir as mybir
from concourse.masks import make_identity

FLOPS = 3 * 2 * 1024 * 1024 * 1024

F32 = mybir.dt.float32
BF16 = mybir.dt.bfloat16
U32 = mybir.dt.uint32
U8 = mybir.dt.uint8
E4 = mybir.dt.float8_e4m3fn_x4
E5 = mybir.dt.float8_e5m2_x4
ALU = mybir.AluOpType

P = 128
U = 1024
HALF = 512
GROUP = 2048
DMA_ALIGN = 2048


def tile_sparsefactorisationdense_pa_v_kernel(
    tc, h0, k1, k2, m1, m2, scaling, bias, z, grad_out, out_0, out_1
):
    nc = tc.nc

    def by_slots(x):
        return x.rearrange("(c p s) w -> c p s w", p=P, s=4)

    def by_pairs(x):
        return x.rearrange("(c a p e) w -> c p a e w", p=P, a=2, e=2)

    k_v = {1: by_pairs(k1), 2: by_slots(k2)}
    m_v = {1: by_pairs(m1), 2: by_slots(m2)}
    z_v, g_v, h_v = by_slots(z), by_slots(grad_out), by_slots(h0)
    out_0_v, out_1_v = by_slots(out_0), by_pairs(out_1)

    with ExitStack() as ctx:
        const = ctx.enter_context(tc.tile_pool(name="const", bufs=1))
        big = ctx.enter_context(tc.tile_pool(name="big", bufs=13))
        small = ctx.enter_context(tc.tile_pool(name="small", bufs=4))
        mask_pool = ctx.enter_context(tc.tile_pool(name="mask_pool", bufs=2))
        prods = ctx.enter_context(tc.tile_pool(name="prods", bufs=3))
        groups = ctx.enter_context(tc.tile_pool(name="groups", bufs=7))
        keep = ctx.enter_context(tc.tile_pool(name="keep", bufs=1))
        psum = ctx.enter_context(tc.psum_pool(name="psum", bufs=8))

        ident = const.tile([P, P], F32, name="ident")
        make_identity(nc, ident[:])
        ones = const.tile([P, P], BF16, name="ones")
        nc.gpsimd.memset(ones[:], 1.0)
        gain_in = const.tile([P, 1], BF16, name="gain_in")
        nc.scalar.dma_start(out=gain_in[0:1, :], in_=scaling.rearrange("(p w) -> p w", p=1))
        gain_row = const.tile([P, 64], BF16, name="gain_row")
        nc.gpsimd.memset(gain_row[:], 0.0)
        gain = const.tile([P, 1], F32, name="gain")

        def codes(name):
            return (
                keep.tile([P, 4, HALF], U32, align_bytes=64, name=name + "_q"),
                keep.tile([P, 4, HALF], U8, align_bytes=64, name=name + "_s"),
            )

        w_codes = {1: codes("w1"), 2: codes("w2")}
        row_codes, db_codes, h_codes = codes("rows"), codes("db"), codes("h")
        dz1 = {(b, jh): keep.tile([P, 4, HALF], BF16, name="dz1_%d%d" % (b, jh)) for b in range(2) for jh in range(2)}

        def bank():
            return psum.tile([P, HALF], F32, name="bank")

        raw, prod, grp, res = {}, {}, {}, {}

        def new_group(key):
            grp[key] = groups.tile([P, GROUP], BF16, align_bytes=64, tag="group", name="g_" + "".join(str(x) for x in key))

        def load(pool, slots, dtype, src, name="raw"):
            t = pool.tile([P, slots, U], dtype, align_bytes=DMA_ALIGN, tag="raw", name=name)
            nc.sync.dma_start(out=t[:] if len(src.shape) == 3 else t[:].rearrange("p (a e) w -> p a e w", e=2), in_=src)
            return t

        def sort_mult(a, b):
            dst = prods.tile([P, 2, 2, HALF], BF16, name="prod")
            nc.vector.tensor_tensor(
                out=dst[:].rearrange("p u a (q r) -> p u (a q) r", r=16),
                in0=a.rearrange("p a (q u r) -> p u (a q) r", u=2, r=16),
                in1=b.rearrange("p a (q u r) -> p u (a q) r", u=2, r=16),
                op=ALU.mult,
            )
            return dst

        def move(out, in_, on):
            if on == "V":
                nc.vector.tensor_copy(out=out, in_=in_)
            else:
                nc.scalar.copy(out=out, in_=in_)

        def turn(parts):
            tr = bank()
            for k, part in enumerate(parts):
                nc.tensor.transpose(tr[:, P * k : P * k + P], part.bitcast(F32), ident[:])
            return tr

        def quantize(pair, k, src, fmt):
            nc.vector.quantize_mx(out=pair[0][:, k, :].bitcast(fmt), scales=pair[1][:, k, :], in_=src[:])

        def product(left, left_fmt, right, right_fmt):
            acc = bank()
            for g in range(2):
                nc.tensor.matmul_mx(
                    out=acc[:],
                    lhsT=left(0, g).bitcast(left_fmt),
                    lhsT_scale=left(1, g),
                    rhs=right(0, g).bitcast(right_fmt),
                    rhs_scale=right(1, g),
                    start=(g == 0),
                    stop=(g == 1),
                )
            return acc


        def ld_w(f, half):
            raw_m = load(big, 4, BF16, m_v[f][half], "m%d%d" % (f, half))
            raw_k = load(big, 4, BF16, k_v[f][half], "k%d%d" % (f, half))
            for pair in range(2):
                raw["m", f, half, pair] = raw_m[:, 2 * pair : 2 * pair + 2, :]
                raw["k", f, half, pair] = raw_k[:, 2 * pair : 2 * pair + 2, :]

        def ld_w_pair(f, half, pair):
            raw["m", f, half, pair] = load(small, 2, BF16, m_v[f][half][:, 2 * pair : 2 * pair + 2, :])[:]
            raw["k", f, half, pair] = load(small, 2, BF16, k_v[f][half][:, 2 * pair : 2 * pair + 2, :])[:]

        def ld_z(n):
            lo = 2 * (n % 2)
            raw["z", n] = load(big, 2, F32, z_v[n // 2][:, lo : lo + 2, :], "z%d" % n)
            raw["g", n] = load(small, 2, BF16, g_v[n // 2][:, lo : lo + 2, :], "g%d" % n)

        def ld_zz(n):
            lo = 2 * (n % 2)
            raw["z", n] = load(big, 2, F32, z_v[n // 2][:, lo : lo + 2, :], "z%d" % n)

        def ld_g(b):
            both = load(big, 4, BF16, g_v[b], "g%d" % b)
            for i in range(2):
                raw["g", 2 * b + i] = both[:, 2 * i : 2 * i + 2, :]

        def ld_h(b):
            raw["h", b] = load(big, 4, BF16, h_v[b], "h%d" % b)

        def wm(f, half, pair):
            prod["w", f, half, pair] = sort_mult(raw["k", f, half, pair], raw["m", f, half, pair])

        def wt(f, half, pair, on="SS", gs=(0, 1)):
            src = prod["w", f, half, pair]
            for g in gs:
                if ("w", f, half, g) not in grp:
                    new_group(("w", f, half, g))
                tr = turn([src[:, u, a, 256 * g : 256 * g + 256] for a in range(2) for u in range(2)])
                words = grp["w", f, half, g][:].bitcast(F32)
                if f == 2:
                    words = words.rearrange("p (r a u) -> p r a u", a=4, u=2)[:, :, 2 * pair : 2 * pair + 2, :]
                    move(words, tr[:].rearrange("p (a u r) -> p r a u", a=2, u=2), on[g])
                else:
                    words = words[:, HALF * pair : HALF * pair + HALF].rearrange("p (r a u) -> p r a u", a=2, u=2)
                    move(words, tr[:].rearrange("p (a u r) -> p r a u", a=2, u=2), on[g])

        def wq(f, half, gs=(0, 1)):
            for g in gs:
                quantize(w_codes[f], 2 * half + g, grp["w", f, half, g], E4)

        def rows_turn(kind, n, part, on, tiles):
            if (kind, n) not in grp:
                new_group((kind, n))
            for i in tiles:
                tr = turn([part(i, g, u) for g in range(2) for u in range(2)])
                words = grp[kind, n][:].bitcast(F32)[:, HALF * i : HALF * i + HALF]
                move(
                    words.rearrange("p (g r u) -> p g r u", g=2, u=2),
                    tr[:].rearrange("p (g u r) -> p g r u", g=2, u=2),
                    on[i],
                )

        def rows_left(n, i):
            return lambda k, g: row_codes[k][:, n, 256 * i + P * g : 256 * i + P * g + P]

        def zs(n):
            mask = mask_pool.tile([P, 2, U], BF16, name="mask")
            nc.vector.tensor_scalar(out=mask[:], in0=raw["z", n][:], scalar1=0.0, scalar2=gain[:], op0=ALU.is_gt, op1=ALU.mult)
            prod["mask", n] = mask

        def zm(n):
            prod["z", n] = sort_mult(raw["g", n][:], prod["mask", n][:])

        def zt(n, on="SS", tiles=(0, 1)):
            rows_turn("z", n, lambda i, g, u: prod["z", n][:, u, i, 256 * g : 256 * g + 256], on, tiles)

        def zq(n):
            quantize(row_codes, n, grp["z", n], E5)

        def p1(n, jh, on="SS", tiles=(0, 1)):
            for i in tiles:
                acc = product(rows_left(n, i), E5, lambda k, g: w_codes[2][k][:, 2 * jh + g, :], E4)
                move(
                    dz1[n // 2, jh][:, 2 * (n % 2) + i, :].rearrange("p (u q r) -> p u q r", u=2, q=16),
                    acc[:].rearrange("p (q u r) -> p u q r", u=2, q=16),
                    on[i],
                )

        def tt(n, on="SS", tiles=(0, 1)):
            rows_turn("t", n, lambda i, g, u: dz1[n // 2, g][:, 2 * (n % 2) + i, 256 * u : 256 * u + 256], on, tiles)

        def tq(n):
            quantize(row_codes, n, grp["t", n], E5)

        def bl(b, jh, on):
            new_group(("b", b, jh))
            move(
                grp["b", b, jh][:].rearrange("p (c i s) -> p c s i", s=4, i=4),
                dz1[b, jh][:].rearrange("p s (c i) -> p c s i", i=4),
                on,
            )

        def bq(b, jh):
            quantize(db_codes, 2 * jh + b, grp["b", b, jh], E5)

        def hl(ih, ah, b, on):
            if ("h", ih, ah) not in grp:
                new_group(("h", ih, ah))
            dst = grp["h", ih, ah][:, U * b : U * b + U]
            lo = HALF * ih + 256 * ah
            src = raw["h", b][:, :, lo : lo + 256]
            move(
                dst.rearrange("p (e c i s) -> p c s i e", e=2, i=2, s=4),
                src.rearrange("p s (c i e) -> p c s i e", i=2, e=2),
                on,
            )

        def hq(ih, ah):
            quantize(h_codes, 2 * ih + ah, grp["h", ih, ah], E4)

        def result(key):
            if key not in res:
                res[key] = big.tile([P, 2, U], F32, align_bytes=DMA_ALIGN, tag="raw", name="r" + "".join(str(x) for x in key))
            return res[key]

        def p3(ih, a, jh):
            acc = product(
                lambda k, b: h_codes[k][:, 2 * ih + a // 2, 256 * b + P * (a % 2) : 256 * b + P * (a % 2) + P], E4,
                lambda k, b: db_codes[k][:, 2 * jh + b, :], E5,
            )
            cols = slice(HALF * jh, HALF * jh + HALF)
            nc.vector.tensor_tensor(
                out=result((1, ih, a // 2))[:, a % 2, cols].rearrange("p (q u r) -> p q u r", u=2, q=16),
                in0=acc[:].rearrange("p (u q r) -> p q u r", u=2, q=16),
                in1=raw["m", 1, ih, a // 2][:, a % 2, cols].rearrange("p (q u r) -> p q u r", u=2, q=16),
                op=ALU.mult,
            )

        def p2(ih, n, on="SS", tiles=(0, 1)):
            for i in tiles:
                acc = product(rows_left(n, i), E5, lambda k, g: w_codes[1][k][:, 2 * ih + g, :], E4)
                move(result((0, n // 2, n % 2))[:, i, HALF * ih : HALF * ih + HALF], acc[:], on[i])

        def st(which, c, pair, slots=slice(0, 2), cols=slice(0, U), queue=nc.sync):
            dst = out_1_v[c][:, pair] if which else out_0_v[c][:, 2 * pair : 2 * pair + 2, :]
            queue.dma_start(out=dst[:, slots, cols], in_=res[which, c, pair][:, slots, cols])

        def spread_gain():
            nc.scalar.copy(out=gain_row[0:1, 0:1], in_=gain_in[0:1, :])
            spread = bank()
            nc.tensor.matmul(spread[:, 0:64], lhsT=ones[:], rhs=gain_row[:], start=True, stop=True)
            nc.scalar.copy(out=gain[:], in_=spread[:, 0:1])

        with tc.manual_schedule():
            ld_w(2,0)
            ld_z(0)
            ld_w(2,1)
            ld_z(1)
            ld_z(2)
            ld_z(3)
            ld_w(1,0)
            ld_w(1,1)
            ld_h(0)
            ld_h(1)
            spread_gain()
            wm(2,0,0)
            wt(2,0,0)
            wm(2,0,1)
            wt(2,0,1)
            zs(0)
            zm(0)
            zt(0)
            wq(2,0)
            zq(0)
            wm(2,1,0)
            wm(2,1,1)
            wt(2,1,0)
            wt(2,1,1)
            p1(0,0)
            zs(1)
            zm(1)
            wq(2,1)
            zt(1)
            p1(0,1)
            zs(2)
            zq(1)
            zm(2)
            tt(0)
            p1(1,0)
            zt(2)
            p1(1,1)
            zs(3)
            tq(0)
            zm(3)
            zq(2)
            zt(3)
            bl(0,0,"V")
            bl(0,1,"V")
            p1(2,0)
            zq(3)
            p1(2,1)
            wm(1,0,0)
            wm(1,0,1)
            tt(1)
            p1(3,0)
            wt(1,0,0)
            wt(1,0,1)
            bq(0,0)
            tq(1)
            bq(0,1)
            wm(1,1,0)
            wm(1,1,1)
            wq(1,0)
            tt(2)
            p1(3,1)
            wt(1,1,0)
            wt(1,1,1,"VS")
            p2(0,0)
            st(0,0,0,slice(0,2),slice(0,HALF))
            tq(2)
            hl(0,0,0,"V")
            hl(0,1,0,"V")
            wq(1,1)
            p2(0,1)
            st(0,0,1,slice(0,2),slice(0,HALF))
            p2(0,2)
            st(0,1,0,slice(0,2),slice(0,HALF))
            bl(1,0,"V")
            tt(3,"VS")
            p2(1,0)
            st(0,0,0,slice(0,2),slice(HALF,U))
            hl(0,0,1,"V")
            hl(0,1,1,"V")
            tq(3)
            hq(0,0)
            bq(1,0)
            bl(1,1,"V")
            p2(1,1)
            st(0,0,1,slice(0,2),slice(HALF,U))
            p2(1,2)
            st(0,1,0,slice(0,2),slice(HALF,U))
            hq(0,1)
            bq(1,1)
            p2(0,3,tiles=(0,))
            p2(1,3,tiles=(0,))
            st(0,1,1,slice(0,1))
            p2(0,3,tiles=(1,))
            p2(1,3,tiles=(1,))
            st(0,1,1,slice(1,2))
            hl(1,0,0,"S")
            hl(1,0,1,"S")
            hl(1,1,0,"S")
            hl(1,1,1,"S")
            p3(0,0,0)
            p3(0,0,1)
            st(1,0,0,slice(0,1))
            p3(0,1,0)
            p3(0,1,1)
            st(1,0,0,slice(1,2))
            p3(0,2,0)
            p3(0,2,1)
            st(1,0,1,slice(0,1))
            hq(1,0)
            p3(0,3,0)
            p3(0,3,1)
            st(1,0,1,slice(1,2))
            p3(1,0,0)
            p3(1,0,1)
            st(1,1,0,slice(0,1))
            hq(1,1)
            p3(1,1,0)
            p3(1,1,1)
            st(1,1,0,slice(1,2),queue=nc.scalar)
            p3(1,2,0)
            p3(1,2,1)
            st(1,1,1,slice(0,1))
            p3(1,3,0)
            p3(1,3,1)
            st(1,1,1,slice(1,2),queue=nc.scalar)
